import numpy as np
import ml_dtypes


def mxq(x, axis, fmt="e4m3"):
    dtype, down = {"e4m3": (ml_dtypes.float8_e4m3fn, 7), "e5m2": (ml_dtypes.float8_e5m2, 14)}[fmt]
    v = np.moveaxis(np.asarray(x, np.float32).astype(ml_dtypes.bfloat16).astype(np.float64), axis, -1)
    blocks = v.reshape(v.shape[:-1] + (-1, 32))
    amax = np.abs(blocks).max(-1, keepdims=True)
    byte = np.maximum(np.where(amax > 0, np.frexp(amax)[1] - 1 + 127, 0) - down, 1)
    scale = np.exp2(byte - 127.0)
    codes = (blocks / scale).astype(np.float32).astype(dtype).astype(np.float64)
    return np.moveaxis((codes * scale).reshape(v.shape), -1, axis)


WIDE = False


def mx_kscale(k):
    if not WIDE:
        return np.ones(k)
    levels = np.array([10, -10, 5, -5, 0])
    if k % 512:
        return np.exp2(np.random.permutation(np.resize(levels, k // 32))).repeat(32)
    a = np.empty((k // 512, 16))
    for p in range(k // 512):
        a[p, :8] = np.random.permutation(np.resize(levels, 8))
        for g in range(8):
            far = levels[np.abs(levels - a[p, g]) >= 10]
            a[p, g + 8] = far[np.random.randint(len(far))]
    return np.exp2(a.ravel()).repeat(32)


BF16 = ml_dtypes.bfloat16


def bf(x):
    return np.asarray(x, np.float32).astype(BF16)


def f64(x):
    return np.asarray(x).astype(np.float64)


B, S, D, H, DN, DR, DV, RQ, RKV = 2, 256, 2048, 16, 64, 128, 128, 1536, 512
THETA = 10000.0
EPS = 1e-6


def rmsnorm(v, w):
    return v * (1.0 / np.sqrt(np.mean(v * v, axis=-1, keepdims=True) + EPS)) * w


def rotate_half(v):
    v1 = v[..., ::2]
    v2 = v[..., 1::2]
    return np.stack((-v2, v1), axis=-1).reshape(v.shape)


def rope_cache():
    inv_freq = 1.0 / THETA ** (np.arange(0, DR, 2) / DR)
    freqs = np.outer(np.arange(S), inv_freq)
    emb = np.concatenate((freqs, freqs), -1)
    return np.cos(emb), np.sin(emb)


def apply_rope(v, cos, sin):
    return v * cos[None, None] + rotate_half(v) * sin[None, None]


def setup_inputs():
    s, t = mx_kscale(D), mx_kscale(RKV)
    return {"x": bf(np.random.standard_normal((B, S, D)) * s),
            "Wkva": bf(np.random.standard_normal((D, RKV + DR)) / np.sqrt(D) / s[:, None]),
            "kv_a_norm_w": bf((1.0 + 0.1 * np.random.standard_normal(RKV)) * t),
            "Wkvb": bf(np.random.standard_normal((RKV, H * (DN + DV))) / np.sqrt(RKV) / t[:, None])}


def reference(x, Wkva, kv_a_norm_w, Wkvb):
    kv_a = mxq(f64(x), 2, "e4m3") @ mxq(f64(Wkva), 0, "e4m3")
    kv_latent, k_rope_shared = kv_a[..., :RKV], kv_a[..., RKV:]
    h = rmsnorm(kv_latent, f64(kv_a_norm_w))
    kv = mxq(h, 2, "e4m3") @ mxq(f64(Wkvb), 0, "e4m3")
    kv = kv.reshape(B, S, H, DN + DV).transpose(0, 2, 1, 3)
    k_nope, v = kv[..., :DN], kv[..., DN:]
    cos, sin = rope_cache()
    k_rope = apply_rope(k_rope_shared[:, None], cos, sin)
    k_rope = np.broadcast_to(k_rope, (B, H, S, DR))
    k_final = np.concatenate([k_nope, k_rope], -1)
    return k_final, v

@@ -1,0 +1,395 @@
+import math
+from contextlib import ExitStack
+
+import concourse.mybir as mybir
+from concourse.masks import make_identity
+
+F32 = mybir.dt.float32
+BF16 = mybir.dt.bfloat16
+I32 = mybir.dt.int32
+U32 = mybir.dt.uint32
+U8 = mybir.dt.uint8
+FP8X4 = mybir.dt.float8_e4m3fn_x4
+ALU = mybir.AluOpType
+ACT = mybir.ActivationFunctionType
+
+P = 128
+PACK = 4
+K_PASS = P * PACK
+
+BATCH, SEQ, D_MODEL = 2, 256, 2048
+HEADS, D_NOPE, D_ROPE, D_V = 16, 64, 128, 128
+LATENT = 512
+A_COLS = LATENT + D_ROPE
+HEAD_COLS = D_NOPE + D_V
+THETA = 10000.0
+EPS = 1e-6
+
+A_PASSES = D_MODEL // K_PASS
+ROWS = SEQ // P
+TILES = BATCH * ROWS
+GROUP_HEADS = 4
+GROUPS = HEADS // GROUP_HEADS
+GROUP_COLS = GROUP_HEADS * HEAD_COLS
+V_COLS = GROUP_HEADS * D_V
+NOPE_COLS = GROUP_HEADS * D_NOPE
+RUN = 4
+
+ROUND_MAGIC = 1.5 * 2.0**23
+COS, SIN = 0, 1
+
+FLOPS = 2 * BATCH * SEQ * (D_MODEL * A_COLS + LATENT * HEADS * HEAD_COLS)
+
+
+def tile_multiheadlatentattention_pb_kernel(tc, x, Wkva, kv_a_norm_w, Wkvb, out_0, out_1):
+    nc = tc.nc
+    with ExitStack() as ctx:
+        const = ctx.enter_context(tc.tile_pool(name="const", bufs=1))
+        raw = ctx.enter_context(tc.tile_pool(name="raw", bufs=1))
+        keep = ctx.enter_context(tc.tile_pool(name="keep", bufs=1))
+        stage = ctx.enter_context(tc.tile_pool(name="stage", bufs=2))
+        per_tile = ctx.enter_context(tc.tile_pool(name="per_tile", bufs=TILES))
+        psum = ctx.enter_context(tc.psum_pool(name="psum", bufs=8))
+        ctx.enter_context(tc.manual_schedule())
+
+        def quantise(codes, scales, grouped):
+            nc.vector.quantize_mx(out=codes.bitcast(FP8X4), scales=scales, in_=grouped)
+
+        def mx_pass(out, lhs_codes, lhs_scales, rhs_codes, rhs_scales, start, stop):
+            nc.tensor.matmul_mx(
+                out=out,
+                lhsT=lhs_codes.bitcast(FP8X4),
+                lhsT_scale=lhs_scales,
+                rhs=rhs_codes.bitcast(FP8X4),
+                rhs_scale=rhs_scales,
+                start=start,
+                stop=stop,
+            )
+
+        gain_row = const.tile([P, LATENT], BF16)
+        nc.gpsimd.memset(gain_row[:], 0.0)
+        wa_raw = []
+        for c in range(A_PASSES):
+            wa_tile = raw.tile([P, PACK, A_COLS], BF16, name="wa_raw%d" % c)
+            nc.sync.dma_start(
+                out=wa_tile[:],
+                in_=Wkva[c * K_PASS : (c + 1) * K_PASS, :].rearrange("(p t) n -> p t n", t=PACK),
+            )
+            wa_raw.append(wa_tile)
+            if c == 0:
+                nc.sync.dma_start(out=gain_row[0:1, :], in_=kv_a_norm_w.rearrange("(o n) -> o n", o=1))
+        x_raw = []
+        for b in range(BATCH):
+            for j in range(ROWS):
+                x_tile = raw.tile([P, D_MODEL], BF16, name="x_raw%d%d" % (b, j))
+                nc.sync.dma_start(out=x_tile[:], in_=x[b].rearrange("(p j) d -> p j d", j=ROWS)[:, j, :])
+                x_raw.append(x_tile)
+        wb_raw = []
+        for g in range(GROUPS):
+            wb_tile = raw.tile([P, PACK, GROUP_COLS], BF16, name="wb_raw%d" % g)
+            nc.sync.dma_start(
+                out=wb_tile[:],
+                in_=Wkvb[:, g * GROUP_COLS : (g + 1) * GROUP_COLS].rearrange("(p t) n -> p t n", t=PACK),
+            )
+            wb_raw.append(wb_tile)
+
+        ident_f32 = const.tile([P, P], F32)
+        make_identity(nc, ident_f32[:])
+        pos_int = const.tile([P, ROWS], I32)
+        nc.gpsimd.iota(pos_int[:], pattern=[[1, ROWS]], base=0, channel_multiplier=ROWS)
+        minus_half = const.tile([P, 1], F32)
+        nc.gpsimd.memset(minus_half[:], -0.5)
+        zero_col = const.tile([P, 1], F32)
+        nc.gpsimd.memset(zero_col[:], 0.0)
+
+        warm = const.tile([P, 1], F32)
+        nc.scalar.activation(out=warm[:], in_=zero_col[:], func=ACT.Sin)
+
+        ones = const.tile([P, P], BF16)
+        nc.vector.memset(ones[:], 1.0)
+        gain_ps = psum.tile([P, LATENT], F32, tag="bank")
+        nc.tensor.matmul(out=gain_ps[:], lhsT=ones[:], rhs=gain_row[:], start=True, stop=True)
+        gain = const.tile([P, LATENT], F32)
+        nc.scalar.copy(out=gain[:], in_=gain_ps[:])
+
+        per_pos = const.tile([P, D_ROPE], F32)
+        nc.vector.memset(per_pos[:], 1.0)
+        for level in range(6):
+            bit = 2**level
+            has_bit = per_pos[:].rearrange("p (a two c) -> p a two c", two=2, c=bit)[:, :, 1, :]
+            nc.vector.tensor_scalar_mul(out=has_bit, in0=has_bit, scalar1=THETA ** (-bit / 64.0))
+        pos = const.tile([P, ROWS], F32)
+        nc.vector.tensor_copy(out=pos[:], in_=pos_int[:])
+        pos_turns = const.tile([P, ROWS], F32)
+        nc.vector.tensor_scalar_mul(out=pos_turns[:], in0=pos[:], scalar1=1.0 / (2.0 * math.pi))
+        turns = const.tile([P, 2, ROWS, D_ROPE], F32)
+        for j in range(ROWS):
+            nc.vector.tensor_scalar(
+                out=turns[:, COS, j, :], in0=per_pos[:], scalar1=pos_turns[:, j : j + 1], scalar2=0.25,
+                op0=ALU.mult, op1=ALU.add,
+            )
+            nc.vector.tensor_scalar(
+                out=turns[:, SIN, j, :], in0=per_pos[:], scalar1=pos_turns[:, j : j + 1], scalar2=None,
+                op0=ALU.mult,
+            )
+        whole = const.tile([P, 2, ROWS, D_ROPE], F32)
+        nc.vector.tensor_scalar(
+            out=whole[:], in0=turns[:], scalar1=ROUND_MAGIC, scalar2=ROUND_MAGIC, op0=ALU.add, op1=ALU.subtract
+        )
+        part = const.tile([P, 2, ROWS, D_ROPE], F32)
+        nc.vector.tensor_tensor(out=part[:], in0=turns[:], in1=whole[:], op=ALU.subtract)
+        sin_even = part[:, SIN, :, :].rearrange("p j (m e) -> p (j m) e", e=2)[:, :, 0]
+        nc.vector.tensor_scalar_mul(out=sin_even, in0=sin_even, scalar1=-1.0)
+        table = const.tile([P, 2, ROWS, D_ROPE], F32)
+
+        x_codes = keep.tile([P, TILES, A_PASSES * P], U32, align_bytes=64)
+        x_scales = keep.tile([P, TILES, A_PASSES * P], U8, align_bytes=64)
+        wa_codes = keep.tile([P, A_PASSES, A_COLS], U32, align_bytes=64)
+        wa_scales = keep.tile([P, A_PASSES, A_COLS], U8, align_bytes=64)
+        h_codes = keep.tile([P, TILES * P], U32, align_bytes=64)
+        h_scales = keep.tile([P, TILES * P], U8, align_bytes=64)
+        wv_codes = keep.tile([P, GROUPS, V_COLS], U32, align_bytes=64)
+        wv_scales = keep.tile([P, GROUPS, V_COLS], U8, align_bytes=64)
+        wn_codes = keep.tile([P, GROUPS, NOPE_COLS], U32, align_bytes=64)
+        wn_scales = keep.tile([P, GROUPS, NOPE_COLS], U8, align_bytes=64)
+
+        HALF_COLS = A_COLS // 2
+
+        def regroup_wa(c):
+            grouped = stage.tile([P, A_COLS, PACK], BF16, align_bytes=64, name="wa_grouped%d" % c, tag="wa_grouped")
+            nc.vector.tensor_copy(
+                out=grouped[:, 0:HALF_COLS, :].rearrange("p (c i) t -> p c t i", i=RUN),
+                in_=wa_raw[c][:, :, 0:HALF_COLS].rearrange("p t (c i) -> p c t i", i=RUN),
+            )
+            nc.scalar.copy(
+                out=grouped[:, HALF_COLS:A_COLS, :].rearrange("p (c i) t -> p c t i", i=RUN),
+                in_=wa_raw[c][:, :, HALF_COLS:A_COLS].rearrange("p t (c i) -> p c t i", i=RUN),
+            )
+            return grouped
+
+        def quantise_wa(c, grouped):
+            for cols in (slice(0, LATENT), slice(LATENT, A_COLS)):
+                quantise(
+                    wa_codes[:, c, cols], wa_scales[:, c, cols], grouped[:, cols, :].rearrange("p n t -> p (n t)")
+                )
+
+        wa_grouped = [regroup_wa(0)]
+        for c in range(A_PASSES):
+            if c + 1 < A_PASSES:
+                wa_grouped.append(regroup_wa(c + 1))
+            quantise_wa(c, wa_grouped[c])
+
+        for i in range(TILES):
+            x_words = x_raw[i][:].bitcast(F32)
+            x_grouped = per_tile.tile([P, A_PASSES * P * PACK], BF16, align_bytes=64)
+            xg_words = x_grouped[:].bitcast(F32).rearrange("p (c r u) -> p c r u", c=A_PASSES, u=2)
+            for half in range(2):
+                xT = psum.tile([P, 2, 2, P], F32, tag="bank")
+                for c2 in range(2):
+                    for u in range(2):
+                        w0 = (2 * half + c2) * 2 * P
+                        nc.tensor.transpose(xT[:, c2, u, :], x_words[:, w0 + u : w0 + 2 * P : 2], ident_f32[:])
+                nc.scalar.copy(
+                    out=xg_words[:, 2 * half : 2 * half + 2, :, :],
+                    in_=xT[:].rearrange("p c u r -> p c r u"),
+                )
+            quantise(x_codes[:, i, :], x_scales[:, i, :], x_grouped[:])
+
+        nc.scalar.activation(out=table[:], in_=part[:], func=ACT.Sin, scale=2.0 * math.pi)
+
+        latent_ps = {}
+        rope_ps = {}
+        hT_ps = {}
+        grouped_w = {}
+        rotated = {}
+        v_ps = {}
+        nope_ps = {}
+        mean_sq = const.tile([P, TILES], F32)
+        mean_eps = const.tile([P, TILES], F32)
+        rstd = const.tile([P, TILES], F32)
+        h_grouped = keep.tile([P, TILES, P, PACK], BF16, align_bytes=64)
+        k_tiles = []
+        for b in range(BATCH):
+            k_tiles.append(keep.tile([P, GROUP_HEADS, ROWS, D_NOPE + D_ROPE], F32, name="k_tile%d" % b))
+
+        def first_product(out, i, cols):
+            for c in range(A_PASSES):
+                toks = slice(c * P, (c + 1) * P)
+                mx_pass(
+                    out, x_codes[:, i, toks], x_scales[:, i, toks], wa_codes[:, c, cols], wa_scales[:, c, cols],
+                    start=(c == 0), stop=(c == A_PASSES - 1),
+                )
+
+        def latent_passes(i):
+            latent_ps[i] = psum.tile([P, LATENT], F32, tag="bank", name="latent_ps%d" % i)
+            first_product(latent_ps[i][:], i, slice(0, LATENT))
+
+        def rope_passes(b):
+            rope_ps[b] = psum.tile([P, ROWS, D_ROPE], F32, tag="bank", name="rope_ps%d" % b)
+            for j in range(ROWS):
+                first_product(rope_ps[b][:, j, :], b * ROWS + j, slice(LATENT, A_COLS))
+
+        def sum_squares(i):
+            col = slice(i, i + 1)
+            squares = stage.tile([P, LATENT], BF16)
+            nc.scalar.activation(
+                out=squares[:], in_=latent_ps[i][:], func=ACT.Square, scale=1.0 / math.sqrt(LATENT),
+                accum_out=mean_sq[:, col],
+            )
+            nc.gpsimd.tensor_scalar(
+                out=mean_eps[:, col], in0=mean_sq[:, col], scalar1=1.0, scalar2=EPS, op0=ALU.mult, op1=ALU.add
+            )
+            nc.gpsimd.tensor_tensor(out=rstd[:, col], in0=mean_eps[:, col], in1=minus_half[:], op=ALU.pow)
+
+        def scale_and_transpose(i):
+            h = per_tile.tile([P, LATENT], BF16)
+            nc.vector.scalar_tensor_tensor(
+                out=h[:], in0=latent_ps[i][:], scalar=rstd[:, i : i + 1], in1=gain[:], op0=ALU.mult, op1=ALU.mult
+            )
+            h_words = h[:].bitcast(F32)
+            hT_ps[i] = psum.tile([P, 2, P], F32, tag="bank", name="hT_ps%d" % i)
+            for u in range(2):
+                nc.tensor.transpose(hT_ps[i][:, u, :], h_words[:, u : 2 * P : 2], ident_f32[:])
+
+        def copy_h(i):
+            nc.scalar.copy(
+                out=h_grouped[:, i, :, :].rearrange("p r t -> p (r t)").bitcast(F32).rearrange("p (r u) -> p r u", u=2),
+                in_=hT_ps[i][:].rearrange("p u r -> p r u"),
+            )
+
+        def quantise_h(b):
+            toks = slice(b * ROWS * P, (b + 1) * ROWS * P)
+            quantise(
+                h_codes[:, toks], h_scales[:, toks],
+                h_grouped[:, b * ROWS : (b + 1) * ROWS, :, :].rearrange("p i r t -> p (i r t)"),
+            )
+
+        def regroup_wb(g, first_col, cols_per_head, grouped):
+            by_head = wb_raw[g][:].rearrange("p t (h f) -> p h t f", f=HEAD_COLS)
+            nc.vector.tensor_copy(
+                out=grouped[:].rearrange("p (h c i t) -> p h c t i", h=GROUP_HEADS, i=RUN, t=PACK),
+                in_=by_head[:, :, :, first_col : first_col + cols_per_head].rearrange(
+                    "p h t (c i) -> p h c t i", i=RUN
+                ),
+            )
+
+        def regroup_v(g):
+            wv_grouped = stage.tile([P, V_COLS * PACK], BF16, align_bytes=64)
+            regroup_wb(g, D_NOPE, D_V, wv_grouped)
+            grouped_w[("v", g)] = wv_grouped
+
+        def regroup_nope(g):
+            wn_grouped = stage.tile([P, NOPE_COLS * PACK], BF16, align_bytes=64)
+            regroup_wb(g, 0, D_NOPE, wn_grouped)
+            grouped_w[("nope", g)] = wn_grouped
+
+        def quantise_v(g):
+            quantise(wv_codes[:, g, :], wv_scales[:, g, :], grouped_w[("v", g)][:])
+
+        def quantise_nope(g):
+            quantise(wn_codes[:, g, :], wn_scales[:, g, :], grouped_w[("nope", g)][:])
+
+        def rotate(b):
+            r_ps = rope_ps[b][:]
+            by_cos = stage.tile([P, ROWS, D_ROPE], F32)
+            nc.vector.tensor_tensor(out=by_cos[:], in0=r_ps, in1=table[:, COS, :, :], op=ALU.mult)
+            by_sin = stage.tile([P, ROWS, D_ROPE], F32)
+            r_pairs = r_ps.rearrange("p j (m e) -> p (j m) e", e=2)
+            sin_pairs = table[:, SIN, :, :].rearrange("p j (m e) -> p (j m) e", e=2)
+            out_pairs = by_sin[:].rearrange("p j (m e) -> p (j m) e", e=2)
+            for e in range(2):
+                nc.vector.tensor_tensor(
+                    out=out_pairs[:, :, e], in0=r_pairs[:, :, 1 - e], in1=sin_pairs[:, :, e], op=ALU.mult
+                )
+            rotated[b] = keep.tile([P, ROWS, D_ROPE], F32, name="rotated%d" % b)
+            nc.vector.tensor_tensor(out=rotated[b][:], in0=by_cos[:], in1=by_sin[:], op=ALU.add)
+
+        def spread(b):
+            nc.vector.tensor_copy(
+                out=k_tiles[b][:, :, :, D_NOPE:],
+                in_=rotated[b][:].unsqueeze(1).to_broadcast([P, GROUP_HEADS, ROWS, D_ROPE]),
+            )
+
+        def second_product(g, b):
+            nope_ps[(g, b)] = psum.tile([P, ROWS, NOPE_COLS], F32, tag="bank", name="nope_ps%d%d" % (g, b))
+            for j in range(ROWS):
+                toks = slice((b * ROWS + j) * P, (b * ROWS + j + 1) * P)
+                v_ps[(g, b, j)] = psum.tile([P, V_COLS], F32, tag="bank", name="v_ps%d%d%d" % (g, b, j))
+                mx_pass(
+                    v_ps[(g, b, j)][:], h_codes[:, toks], h_scales[:, toks],
+                    wv_codes[:, g, :], wv_scales[:, g, :], start=True, stop=True,
+                )
+            for j in range(ROWS):
+                toks = slice((b * ROWS + j) * P, (b * ROWS + j + 1) * P)
+                mx_pass(
+                    nope_ps[(g, b)][:, j, :], h_codes[:, toks], h_scales[:, toks],
+                    wn_codes[:, g, :], wn_scales[:, g, :], start=True, stop=True,
+                )
+
+        def store_v(g, b):
+            heads = slice(g * GROUP_HEADS, (g + 1) * GROUP_HEADS)
+            v_tile = per_tile.tile([P, GROUP_HEADS, ROWS, D_V], F32)
+            for j in range(ROWS):
+                nc.scalar.copy(
+                    out=v_tile[:, :, j, :], in_=v_ps[(g, b, j)][:].rearrange("p (h f) -> p h f", h=GROUP_HEADS)
+                )
+            nc.sync.dma_start(
+                out=out_1[b, heads].rearrange("h (p j) f -> p h (j f)", j=ROWS),
+                in_=v_tile[:].rearrange("p h j f -> p h (j f)"),
+            )
+
+        def store_k(g, b):
+            heads = slice(g * GROUP_HEADS, (g + 1) * GROUP_HEADS)
+            nc.scalar.copy(
+                out=k_tiles[b][:, :, :, 0:D_NOPE],
+                in_=nope_ps[(g, b)][:].rearrange("p j (h f) -> p h j f", h=GROUP_HEADS),
+            )
+            nc.sync.dma_start(
+                out=out_0[b, heads].rearrange("h (p j) f -> p h (j f)", j=ROWS),
+                in_=k_tiles[b][:].rearrange("p h j f -> p h (j f)"),
+            )
+
+        for i in range(TILES):
+            latent_passes(i)
+        regroup_v(0)
+        quantise_v(0)
+        for i in range(TILES):
+            sum_squares(i)
+        scale_and_transpose(0)
+        regroup_nope(0)
+        scale_and_transpose(1)
+        quantise_nope(0)
+        rope_passes(0)
+        scale_and_transpose(2)
+        scale_and_transpose(3)
+        for i in range(TILES):
+            copy_h(i)
+        quantise_h(0)
+        second_product(0, 0)
+        rotate(0)
+        spread(0)
+        rope_passes(1)
+        quantise_h(1)
+        store_v(0, 0)
+        store_k(0, 0)
+        regroup_v(1)
+        rotate(1)
+        second_product(0, 1)
+        quantise_v(1)
+        spread(1)
+        store_v(0, 1)
+        regroup_nope(1)
+        store_k(0, 1)
+        quantise_nope(1)
+        for g in range(1, GROUPS):
+            for b in range(BATCH):
+                second_product(g, b)
+            if g + 1 < GROUPS:
+                regroup_v(g + 1)
+                regroup_nope(g + 1)
+                quantise_v(g + 1)
+                quantise_nope(g + 1)
+            for b in range(BATCH):
+                store_v(g, b)
+            for b in range(BATCH):
+                store_k(g, b)

@@ -33,6 +33,10 @@ GROUPS = HEADS // GROUP_HEADS
 GROUP_COLS = GROUP_HEADS * HEAD_COLS
 V_COLS = GROUP_HEADS * D_V
 NOPE_COLS = GROUP_HEADS * D_NOPE
+VECTOR_COLS = (384, 256, 256, 256)
+SPLIT_GROUPS = 2
+SPLIT_HEADS = SPLIT_GROUPS * GROUP_HEADS
+FREQS = D_ROPE // 2
 RUN = 4
 
 ROUND_MAGIC = 1.5 * 2.0**23
@@ -49,8 +53,14 @@ def tile_multiheadlatentattention_pb_kernel(tc, x, Wkva, kv_a_norm_w, Wkvb, out_
         keep = ctx.enter_context(tc.tile_pool(name="keep", bufs=1))
         stage = ctx.enter_context(tc.tile_pool(name="stage", bufs=2))
         per_tile = ctx.enter_context(tc.tile_pool(name="per_tile", bufs=TILES))
-        psum = ctx.enter_context(tc.psum_pool(name="psum", bufs=8))
+        psum = ctx.enter_context(tc.psum_pool(name="psum", bufs=1))
         ctx.enter_context(tc.manual_schedule())
+
+        def bank_hold(shape, dtype, name):
+            return psum.tile(shape, dtype, tag="hold", bufs=4, name=name)
+
+        def bank_pass(shape, dtype, name):
+            return psum.tile(shape, dtype, tag="pass", bufs=4, name=name)
 
         def quantise(codes, scales, grouped):
             nc.vector.quantize_mx(out=codes.bitcast(FP8X4), scales=scales, in_=grouped)
@@ -66,81 +76,91 @@ def tile_multiheadlatentattention_pb_kernel(tc, x, Wkva, kv_a_norm_w, Wkvb, out_
                 stop=stop,
             )
 
-        gain_row = const.tile([P, LATENT], BF16)
-        nc.gpsimd.memset(gain_row[:], 0.0)
-        wa_raw = []
-        for c in range(A_PASSES):
-            wa_tile = raw.tile([P, PACK, A_COLS], BF16, name="wa_raw%d" % c)
+        wa_raw = {}
+        x_raw = {}
+        wb_raw = {}
+
+        def load_wa(c):
+            wa_raw[c] = raw.tile([P, PACK, A_COLS], BF16, name="wa_raw%d" % c)
             nc.sync.dma_start(
-                out=wa_tile[:],
-                in_=Wkva[c * K_PASS : (c + 1) * K_PASS, :].rearrange("(p t) n -> p t n", t=PACK),
+                out=wa_raw[c][:], in_=Wkva[c * K_PASS : (c + 1) * K_PASS, :].rearrange("(p t) n -> p t n", t=PACK)
             )
-            wa_raw.append(wa_tile)
-            if c == 0:
-                nc.sync.dma_start(out=gain_row[0:1, :], in_=kv_a_norm_w.rearrange("(o n) -> o n", o=1))
-        x_raw = []
-        for b in range(BATCH):
-            for j in range(ROWS):
-                x_tile = raw.tile([P, D_MODEL], BF16, name="x_raw%d%d" % (b, j))
-                nc.sync.dma_start(out=x_tile[:], in_=x[b].rearrange("(p j) d -> p j d", j=ROWS)[:, j, :])
-                x_raw.append(x_tile)
-        wb_raw = []
-        for g in range(GROUPS):
-            wb_tile = raw.tile([P, PACK, GROUP_COLS], BF16, name="wb_raw%d" % g)
+
+        def load_x(i):
+            b, j = divmod(i, ROWS)
+            x_raw[i] = raw.tile([P, D_MODEL], BF16, name="x_raw%d" % i)
+            nc.sync.dma_start(out=x_raw[i][:], in_=x[b].rearrange("(p j) d -> p j d", j=ROWS)[:, j, :])
+
+        def load_wb(g):
+            wb_raw[g] = raw.tile([P, PACK, GROUP_COLS], BF16, name="wb_raw%d" % g)
             nc.sync.dma_start(
-                out=wb_tile[:],
+                out=wb_raw[g][:],
                 in_=Wkvb[:, g * GROUP_COLS : (g + 1) * GROUP_COLS].rearrange("(p t) n -> p t n", t=PACK),
             )
-            wb_raw.append(wb_tile)
+
+        pos = const.tile([P, ROWS], F32)
+        nc.gpsimd.iota(
+            pos[:], pattern=[[1, ROWS]], base=0, channel_multiplier=ROWS, allow_small_or_imprecise_dtypes=True
+        )
+        zero_col = const.tile([P, 1], F32)
+        nc.gpsimd.memset(zero_col[:], 0.0)
+        ident_bf = const.tile([P, P], BF16)
+        make_identity(nc, ident_bf[:])
+        gain_row = const.tile([P, LATENT], BF16)
+        nc.gpsimd.memset(gain_row[:], 0.0)
+        load_wa(0)
+        load_x(0)
+        load_wa(1)
+        load_x(1)
+        nc.sync.dma_start(out=gain_row[0:1, :], in_=kv_a_norm_w.rearrange("(o n) -> o n", o=1))
+        load_wa(2)
+        load_wa(3)
+        load_x(2)
+        load_x(3)
+        for g in range(GROUPS):
+            load_wb(g)
 
         ident_f32 = const.tile([P, P], F32)
         make_identity(nc, ident_f32[:])
-        pos_int = const.tile([P, ROWS], I32)
-        nc.gpsimd.iota(pos_int[:], pattern=[[1, ROWS]], base=0, channel_multiplier=ROWS)
-        minus_half = const.tile([P, 1], F32)
-        nc.gpsimd.memset(minus_half[:], -0.5)
-        zero_col = const.tile([P, 1], F32)
-        nc.gpsimd.memset(zero_col[:], 0.0)
+        ones = const.tile([P, P], BF16)
+        nc.gpsimd.memset(ones[:], 1.0)
 
         warm = const.tile([P, 1], F32)
         nc.scalar.activation(out=warm[:], in_=zero_col[:], func=ACT.Sin)
-
-        ones = const.tile([P, P], BF16)
-        nc.vector.memset(ones[:], 1.0)
-        gain_ps = psum.tile([P, LATENT], F32, tag="bank")
-        nc.tensor.matmul(out=gain_ps[:], lhsT=ones[:], rhs=gain_row[:], start=True, stop=True)
-        gain = const.tile([P, LATENT], F32)
-        nc.scalar.copy(out=gain[:], in_=gain_ps[:])
-
-        per_pos = const.tile([P, D_ROPE], F32)
+        per_pos = const.tile([P, FREQS], F32)
         nc.vector.memset(per_pos[:], 1.0)
         for level in range(6):
             bit = 2**level
             has_bit = per_pos[:].rearrange("p (a two c) -> p a two c", two=2, c=bit)[:, :, 1, :]
             nc.vector.tensor_scalar_mul(out=has_bit, in0=has_bit, scalar1=THETA ** (-bit / 64.0))
-        pos = const.tile([P, ROWS], F32)
-        nc.vector.tensor_copy(out=pos[:], in_=pos_int[:])
-        pos_turns = const.tile([P, ROWS], F32)
-        nc.vector.tensor_scalar_mul(out=pos_turns[:], in0=pos[:], scalar1=1.0 / (2.0 * math.pi))
-        turns = const.tile([P, 2, ROWS, D_ROPE], F32)
-        for j in range(ROWS):
-            nc.vector.tensor_scalar(
-                out=turns[:, COS, j, :], in0=per_pos[:], scalar1=pos_turns[:, j : j + 1], scalar2=0.25,
-                op0=ALU.mult, op1=ALU.add,
-            )
-            nc.vector.tensor_scalar(
-                out=turns[:, SIN, j, :], in0=per_pos[:], scalar1=pos_turns[:, j : j + 1], scalar2=None,
-                op0=ALU.mult,
-            )
-        whole = const.tile([P, 2, ROWS, D_ROPE], F32)
+        eps_col = const.tile([P, 1], F32)
+        nc.vector.tensor_scalar(out=eps_col[:], in0=zero_col[:], scalar1=1.0, scalar2=EPS, op0=ALU.mult, op1=ALU.add)
+
+        turns = const.tile([P, 2, ROWS, FREQS], F32)
+        nc.vector.scalar_tensor_tensor(
+            out=turns[:, SIN, :, :], in0=per_pos[:].unsqueeze(1).to_broadcast([P, ROWS, FREQS]),
+            scalar=1.0 / (2.0 * math.pi), in1=pos[:].unsqueeze(2).to_broadcast([P, ROWS, FREQS]),
+            op0=ALU.mult, op1=ALU.mult,
+        )
+        nc.vector.tensor_scalar(
+            out=turns[:, COS, :, :], in0=turns[:, SIN, :, :], scalar1=1.0, scalar2=0.25, op0=ALU.mult, op1=ALU.add
+        )
+        whole = const.tile([P, 2, ROWS, FREQS], F32)
         nc.vector.tensor_scalar(
             out=whole[:], in0=turns[:], scalar1=ROUND_MAGIC, scalar2=ROUND_MAGIC, op0=ALU.add, op1=ALU.subtract
         )
-        part = const.tile([P, 2, ROWS, D_ROPE], F32)
+        part = const.tile([P, 2, ROWS, FREQS], F32)
         nc.vector.tensor_tensor(out=part[:], in0=turns[:], in1=whole[:], op=ALU.subtract)
         sin_even = part[:, SIN, :, :].rearrange("p j (m e) -> p (j m) e", e=2)[:, :, 0]
         nc.vector.tensor_scalar_mul(out=sin_even, in0=sin_even, scalar1=-1.0)
         table = const.tile([P, 2, ROWS, D_ROPE], F32)
+        nc.scalar.activation(
+            out=table[:].rearrange("p s j (h f) -> p (s j) h f", h=2),
+            in_=part[:].rearrange("p s j f -> p (s j) f").unsqueeze(2).to_broadcast([P, 2 * ROWS, 2, FREQS]),
+            func=ACT.Sin, scale=2.0 * math.pi,
+        )
+        warm_norm = const.tile([P, 1], F32)
+        nc.scalar.activation(out=warm_norm[:], in_=eps_col[:], func=ACT.Abs_reciprocal_sqrt)
 
         x_codes = keep.tile([P, TILES, A_PASSES * P], U32, align_bytes=64)
         x_scales = keep.tile([P, TILES, A_PASSES * P], U8, align_bytes=64)
@@ -152,82 +172,112 @@ def tile_multiheadlatentattention_pb_kernel(tc, x, Wkva, kv_a_norm_w, Wkvb, out_
         wv_scales = keep.tile([P, GROUPS, V_COLS], U8, align_bytes=64)
         wn_codes = keep.tile([P, GROUPS, NOPE_COLS], U32, align_bytes=64)
         wn_scales = keep.tile([P, GROUPS, NOPE_COLS], U8, align_bytes=64)
+        mean_sq = const.tile([P, TILES], F32)
+        rstd = const.tile([P, TILES], F32)
+        gain = const.tile([P, LATENT], F32)
+        h_grouped = keep.tile([P, TILES, P, PACK], BF16, align_bytes=64)
 
-        HALF_COLS = A_COLS // 2
-
-        def regroup_wa(c):
-            grouped = stage.tile([P, A_COLS, PACK], BF16, align_bytes=64, name="wa_grouped%d" % c, tag="wa_grouped")
-            nc.vector.tensor_copy(
-                out=grouped[:, 0:HALF_COLS, :].rearrange("p (c i) t -> p c t i", i=RUN),
-                in_=wa_raw[c][:, :, 0:HALF_COLS].rearrange("p t (c i) -> p c t i", i=RUN),
-            )
-            nc.scalar.copy(
-                out=grouped[:, HALF_COLS:A_COLS, :].rearrange("p (c i) t -> p c t i", i=RUN),
-                in_=wa_raw[c][:, :, HALF_COLS:A_COLS].rearrange("p t (c i) -> p c t i", i=RUN),
-            )
-            return grouped
-
-        def quantise_wa(c, grouped):
-            for cols in (slice(0, LATENT), slice(LATENT, A_COLS)):
-                quantise(
-                    wa_codes[:, c, cols], wa_scales[:, c, cols], grouped[:, cols, :].rearrange("p n t -> p (n t)")
-                )
-
-        wa_grouped = [regroup_wa(0)]
-        for c in range(A_PASSES):
-            if c + 1 < A_PASSES:
-                wa_grouped.append(regroup_wa(c + 1))
-            quantise_wa(c, wa_grouped[c])
-
-        for i in range(TILES):
-            x_words = x_raw[i][:].bitcast(F32)
-            x_grouped = per_tile.tile([P, A_PASSES * P * PACK], BF16, align_bytes=64)
-            xg_words = x_grouped[:].bitcast(F32).rearrange("p (c r u) -> p c r u", c=A_PASSES, u=2)
-            for half in range(2):
-                xT = psum.tile([P, 2, 2, P], F32, tag="bank")
-                for c2 in range(2):
-                    for u in range(2):
-                        w0 = (2 * half + c2) * 2 * P
-                        nc.tensor.transpose(xT[:, c2, u, :], x_words[:, w0 + u : w0 + 2 * P : 2], ident_f32[:])
-                nc.scalar.copy(
-                    out=xg_words[:, 2 * half : 2 * half + 2, :, :],
-                    in_=xT[:].rearrange("p c u r -> p c r u"),
-                )
-            quantise(x_codes[:, i, :], x_scales[:, i, :], x_grouped[:])
-
-        nc.scalar.activation(out=table[:], in_=part[:], func=ACT.Sin, scale=2.0 * math.pi)
-
+        wa_grouped = {}
+        wa_ps = {}
+        xT_ps = {}
+        x_grouped = {}
         latent_ps = {}
         rope_ps = {}
         hT_ps = {}
-        grouped_w = {}
+        wn_ps = {}
+        wv_grouped = {}
+        wn_grouped = {}
         rotated = {}
         v_ps = {}
         nope_ps = {}
-        mean_sq = const.tile([P, TILES], F32)
-        mean_eps = const.tile([P, TILES], F32)
-        rstd = const.tile([P, TILES], F32)
-        h_grouped = keep.tile([P, TILES, P, PACK], BF16, align_bytes=64)
-        k_tiles = []
+        k_tiles = {}
+        nope_tiles = {}
         for b in range(BATCH):
-            k_tiles.append(keep.tile([P, GROUP_HEADS, ROWS, D_NOPE + D_ROPE], F32, name="k_tile%d" % b))
+            nope_tiles[b] = keep.tile([P, SPLIT_HEADS, ROWS, D_NOPE], F32, name="nope_tile%d" % b)
 
-        def first_product(out, i, cols):
-            for c in range(A_PASSES):
-                toks = slice(c * P, (c + 1) * P)
-                mx_pass(
-                    out, x_codes[:, i, toks], x_scales[:, i, toks], wa_codes[:, c, cols], wa_scales[:, c, cols],
-                    start=(c == 0), stop=(c == A_PASSES - 1),
+        def interleave(out, rhs):
+            for t2 in range(PACK // 2):
+                pair = slice(2 * t2, 2 * t2 + 2)
+                nc.tensor.matmul(
+                    out=out.rearrange("p n t -> p t n")[:, pair, :], lhsT=ident_bf[:], rhs=rhs[:, pair, :],
+                    start=True, stop=True,
                 )
 
-        def latent_passes(i):
-            latent_ps[i] = psum.tile([P, LATENT], F32, tag="bank", name="latent_ps%d" % i)
-            first_product(latent_ps[i][:], i, slice(0, LATENT))
+        def psum_cols(c, half):
+            width = (A_COLS - VECTOR_COLS[c]) // 2
+            first = VECTOR_COLS[c] + half * width
+            return slice(first, first + width)
+
+        def fill_wa(c, half):
+            cols = psum_cols(c, half)
+            wa_ps[(c, half)] = bank_pass([P, cols.stop - cols.start, PACK], BF16, "wa_ps%d%d" % (c, half))
+            interleave(wa_ps[(c, half)][:], wa_raw[c][:, :, cols])
+
+        def regroup_wa(c):
+            wa_grouped[c] = stage.tile([P, A_COLS, PACK], BF16, align_bytes=64, name="wa_grouped%d" % c, tag="wa_grouped")
+            nc.vector.tensor_copy(
+                out=wa_grouped[c][:, 0 : VECTOR_COLS[c], :].rearrange("p (c i) t -> p c t i", i=RUN),
+                in_=wa_raw[c][:, :, 0 : VECTOR_COLS[c]].rearrange("p t (c i) -> p c t i", i=RUN),
+            )
+
+        def copy_wa(c, half):
+            nc.scalar.copy(out=wa_grouped[c][:, psum_cols(c, half), :], in_=wa_ps[(c, half)][:])
+
+        def quantise_wa(c):
+            for cols in (slice(0, LATENT), slice(LATENT, A_COLS)):
+                quantise(
+                    wa_codes[:, c, cols], wa_scales[:, c, cols],
+                    wa_grouped[c][:, cols, :].rearrange("p n t -> p (n t)"),
+                )
+
+        def transpose_x(i):
+            x_words = x_raw[i][:].bitcast(F32)
+            for half in range(2):
+                xT_ps[(i, half)] = bank_pass([P, 2, 2, P], F32, "xT_ps%d%d" % (i, half))
+                for c2 in range(2):
+                    for u in range(2):
+                        w0 = (2 * half + c2) * 2 * P
+                        nc.tensor.transpose(
+                            xT_ps[(i, half)][:, c2, u, :], x_words[:, w0 + u : w0 + 2 * P : 2], ident_f32[:]
+                        )
+
+        def copy_x(i, half):
+            if half == 0:
+                x_grouped[i] = per_tile.tile([P, A_PASSES * P * PACK], BF16, align_bytes=64, name="x_grouped%d" % i, tag="x_grouped")
+            xg_words = x_grouped[i][:].bitcast(F32).rearrange("p (c r u) -> p c r u", c=A_PASSES, u=2)
+            nc.scalar.copy(
+                out=xg_words[:, 2 * half : 2 * half + 2, :, :],
+                in_=xT_ps[(i, half)][:].rearrange("p c u r -> p c r u"),
+            )
+
+        def quantise_x(i):
+            quantise(x_codes[:, i, :], x_scales[:, i, :], x_grouped[i][:])
+
+        def spread_gain():
+            gain_ps = bank_pass([P, LATENT], F32, "gain_ps")
+            nc.tensor.matmul(out=gain_ps[:], lhsT=ones[:], rhs=gain_row[:], start=True, stop=True)
+            nc.scalar.copy(out=gain[:], in_=gain_ps[:])
+
+        def latent_pass(c, i):
+            if c == 0:
+                latent_ps[i] = bank_hold([P, LATENT], F32, "latent_ps%d" % i)
+            toks = slice(c * P, (c + 1) * P)
+            mx_pass(
+                latent_ps[i][:], x_codes[:, i, toks], x_scales[:, i, toks],
+                wa_codes[:, c, 0:LATENT], wa_scales[:, c, 0:LATENT], start=(c == 0), stop=(c == A_PASSES - 1),
+            )
 
         def rope_passes(b):
-            rope_ps[b] = psum.tile([P, ROWS, D_ROPE], F32, tag="bank", name="rope_ps%d" % b)
+            rope_ps[b] = bank_hold([P, ROWS, D_ROPE], F32, "rope_ps%d" % b)
             for j in range(ROWS):
-                first_product(rope_ps[b][:, j, :], b * ROWS + j, slice(LATENT, A_COLS))
+                i = b * ROWS + j
+                for c in range(A_PASSES):
+                    toks = slice(c * P, (c + 1) * P)
+                    mx_pass(
+                        rope_ps[b][:, j, :], x_codes[:, i, toks], x_scales[:, i, toks],
+                        wa_codes[:, c, LATENT:A_COLS], wa_scales[:, c, LATENT:A_COLS],
+                        start=(c == 0), stop=(c == A_PASSES - 1),
+                    )
 
         def sum_squares(i):
             col = slice(i, i + 1)
@@ -236,10 +286,9 @@ def tile_multiheadlatentattention_pb_kernel(tc, x, Wkva, kv_a_norm_w, Wkvb, out_
                 out=squares[:], in_=latent_ps[i][:], func=ACT.Square, scale=1.0 / math.sqrt(LATENT),
                 accum_out=mean_sq[:, col],
             )
-            nc.gpsimd.tensor_scalar(
-                out=mean_eps[:, col], in0=mean_sq[:, col], scalar1=1.0, scalar2=EPS, op0=ALU.mult, op1=ALU.add
+            nc.scalar.activation(
+                out=rstd[:, col], in_=mean_sq[:, col], func=ACT.Abs_reciprocal_sqrt, bias=eps_col[:], scale=1.0
             )
-            nc.gpsimd.tensor_tensor(out=rstd[:, col], in0=mean_eps[:, col], in1=minus_half[:], op=ALU.pow)
 
         def scale_and_transpose(i):
             h = per_tile.tile([P, LATENT], BF16)
@@ -247,7 +296,7 @@ def tile_multiheadlatentattention_pb_kernel(tc, x, Wkva, kv_a_norm_w, Wkvb, out_
                 out=h[:], in0=latent_ps[i][:], scalar=rstd[:, i : i + 1], in1=gain[:], op0=ALU.mult, op1=ALU.mult
             )
             h_words = h[:].bitcast(F32)
-            hT_ps[i] = psum.tile([P, 2, P], F32, tag="bank", name="hT_ps%d" % i)
+            hT_ps[i] = bank_pass([P, 2, P], F32, "hT_ps%d" % i)
             for u in range(2):
                 nc.tensor.transpose(hT_ps[i][:, u, :], h_words[:, u : 2 * P : 2], ident_f32[:])
 
@@ -264,30 +313,45 @@ def tile_multiheadlatentattention_pb_kernel(tc, x, Wkva, kv_a_norm_w, Wkvb, out_
                 h_grouped[:, b * ROWS : (b + 1) * ROWS, :, :].rearrange("p i r t -> p (i r t)"),
             )
 
-        def regroup_wb(g, first_col, cols_per_head, grouped):
+        def fill_nope(g):
+            wn_ps[g] = bank_pass([P, NOPE_COLS, PACK], BF16, "wn_ps%d" % g)
+            by_head = wb_raw[g][:].rearrange("p t (h f) -> p t h f", f=HEAD_COLS)
+            for t2 in range(PACK // 2):
+                for h2 in range(2):
+                    pair = slice(2 * t2, 2 * t2 + 2)
+                    nc.tensor.matmul(
+                        out=wn_ps[g][:].rearrange("p (h f) t -> p t h f", f=D_NOPE)[:, pair, 2 * h2 : 2 * h2 + 2, :],
+                        lhsT=ident_bf[:], rhs=by_head[:, pair, 2 * h2 : 2 * h2 + 2, 0:D_NOPE], start=True, stop=True,
+                    )
+
+        def group_nope(g):
+            wn_grouped[g] = stage.tile([P, NOPE_COLS, PACK], BF16, align_bytes=64, name="wn_grouped%d" % g, tag="wn_grouped")
+
+        def copy_nope(g):
+            group_nope(g)
+            nc.scalar.copy(out=wn_grouped[g][:], in_=wn_ps[g][:])
+
+        def regroup_nope(g):
+            group_nope(g)
             by_head = wb_raw[g][:].rearrange("p t (h f) -> p h t f", f=HEAD_COLS)
             nc.vector.tensor_copy(
-                out=grouped[:].rearrange("p (h c i t) -> p h c t i", h=GROUP_HEADS, i=RUN, t=PACK),
-                in_=by_head[:, :, :, first_col : first_col + cols_per_head].rearrange(
-                    "p h t (c i) -> p h c t i", i=RUN
-                ),
+                out=wn_grouped[g][:].rearrange("p (h c i) t -> p h c t i", h=GROUP_HEADS, i=RUN),
+                in_=by_head[:, :, :, 0:D_NOPE].rearrange("p h t (c i) -> p h c t i", i=RUN),
             )
 
         def regroup_v(g):
-            wv_grouped = stage.tile([P, V_COLS * PACK], BF16, align_bytes=64)
-            regroup_wb(g, D_NOPE, D_V, wv_grouped)
-            grouped_w[("v", g)] = wv_grouped
-
-        def regroup_nope(g):
-            wn_grouped = stage.tile([P, NOPE_COLS * PACK], BF16, align_bytes=64)
-            regroup_wb(g, 0, D_NOPE, wn_grouped)
-            grouped_w[("nope", g)] = wn_grouped
+            wv_grouped[g] = stage.tile([P, V_COLS * PACK], BF16, align_bytes=64, name="wv_grouped%d" % g, tag="wv_grouped")
+            by_head = wb_raw[g][:].rearrange("p t (h f) -> p h t f", f=HEAD_COLS)
+            nc.vector.tensor_copy(
+                out=wv_grouped[g][:].rearrange("p (h c i t) -> p h c t i", h=GROUP_HEADS, i=RUN, t=PACK),
+                in_=by_head[:, :, :, D_NOPE:].rearrange("p h t (c i) -> p h c t i", i=RUN),
+            )
 
         def quantise_v(g):
-            quantise(wv_codes[:, g, :], wv_scales[:, g, :], grouped_w[("v", g)][:])
+            quantise(wv_codes[:, g, :], wv_scales[:, g, :], wv_grouped[g][:])
 
         def quantise_nope(g):
-            quantise(wn_codes[:, g, :], wn_scales[:, g, :], grouped_w[("nope", g)][:])
+            quantise(wn_codes[:, g, :], wn_scales[:, g, :], wn_grouped[g][:].rearrange("p n t -> p (n t)"))
 
         def rotate(b):
             r_ps = rope_ps[b][:]
@@ -304,23 +368,49 @@ def tile_multiheadlatentattention_pb_kernel(tc, x, Wkva, kv_a_norm_w, Wkvb, out_
             rotated[b] = keep.tile([P, ROWS, D_ROPE], F32, name="rotated%d" % b)
             nc.vector.tensor_tensor(out=rotated[b][:], in0=by_cos[:], in1=by_sin[:], op=ALU.add)
 
-        def spread(b):
+        def spread(b, n):
+            k_tiles[(b, n)] = keep.tile([P, GROUP_HEADS, ROWS, D_NOPE + D_ROPE], F32, name="k_tile%d%d" % (b, n))
             nc.vector.tensor_copy(
-                out=k_tiles[b][:, :, :, D_NOPE:],
+                out=k_tiles[(b, n)][:, :, :, D_NOPE:],
                 in_=rotated[b][:].unsqueeze(1).to_broadcast([P, GROUP_HEADS, ROWS, D_ROPE]),
             )
 
-        def second_product(g, b):
-            nope_ps[(g, b)] = psum.tile([P, ROWS, NOPE_COLS], F32, tag="bank", name="nope_ps%d%d" % (g, b))
+        def store_rope(b):
             for j in range(ROWS):
-                toks = slice((b * ROWS + j) * P, (b * ROWS + j + 1) * P)
-                v_ps[(g, b, j)] = psum.tile([P, V_COLS], F32, tag="bank", name="v_ps%d%d%d" % (g, b, j))
+                nc.sync.dma_start(
+                    out=out_0[b, 0:SPLIT_HEADS].rearrange("h (p j) f -> p h j f", j=ROWS)[:, :, j, D_NOPE:],
+                    in_=rotated[b][:, j, :].unsqueeze(1).to_broadcast([P, SPLIT_HEADS, D_ROPE]),
+                )
+
+        def copy_n(g, b):
+            nc.scalar.copy(
+                out=nope_tiles[b][:, g * GROUP_HEADS : (g + 1) * GROUP_HEADS, :, :],
+                in_=nope_ps[(g, b)][:].rearrange("p j (h f) -> p h j f", h=GROUP_HEADS),
+            )
+
+        def store_nope(b):
+            for j in range(ROWS):
+                nc.sync.dma_start(
+                    out=out_0[b, 0:SPLIT_HEADS].rearrange("h (p j) f -> p h j f", j=ROWS)[:, :, j, 0:D_NOPE],
+                    in_=nope_tiles[b][:, :, j, :],
+                )
+
+        def tokens(b, j):
+            return slice((b * ROWS + j) * P, (b * ROWS + j + 1) * P)
+
+        def product_v(g, b):
+            for j in range(ROWS):
+                toks = tokens(b, j)
+                v_ps[(g, b, j)] = bank_pass([P, V_COLS], F32, "v_ps%d%d%d" % (g, b, j))
                 mx_pass(
                     v_ps[(g, b, j)][:], h_codes[:, toks], h_scales[:, toks],
                     wv_codes[:, g, :], wv_scales[:, g, :], start=True, stop=True,
                 )
+
+        def product_nope(g, b):
+            nope_ps[(g, b)] = bank_hold([P, ROWS, NOPE_COLS], F32, "nope_ps%d%d" % (g, b))
             for j in range(ROWS):
-                toks = slice((b * ROWS + j) * P, (b * ROWS + j + 1) * P)
+                toks = tokens(b, j)
                 mx_pass(
                     nope_ps[(g, b)][:, j, :], h_codes[:, toks], h_scales[:, toks],
                     wn_codes[:, g, :], wn_scales[:, g, :], start=True, stop=True,
@@ -340,56 +430,125 @@ def tile_multiheadlatentattention_pb_kernel(tc, x, Wkva, kv_a_norm_w, Wkvb, out_
 
         def store_k(g, b):
             heads = slice(g * GROUP_HEADS, (g + 1) * GROUP_HEADS)
+            k_tile = k_tiles[(b, g % 2)]
             nc.scalar.copy(
-                out=k_tiles[b][:, :, :, 0:D_NOPE],
+                out=k_tile[:, :, :, 0:D_NOPE],
                 in_=nope_ps[(g, b)][:].rearrange("p j (h f) -> p h j f", h=GROUP_HEADS),
             )
             nc.sync.dma_start(
                 out=out_0[b, heads].rearrange("h (p j) f -> p h (j f)", j=ROWS),
-                in_=k_tiles[b][:].rearrange("p h j f -> p h (j f)"),
+                in_=k_tile[:].rearrange("p h j f -> p h (j f)"),
             )
 
-        for i in range(TILES):
-            latent_passes(i)
-        regroup_v(0)
-        quantise_v(0)
-        for i in range(TILES):
-            sum_squares(i)
-        scale_and_transpose(0)
-        regroup_nope(0)
-        scale_and_transpose(1)
-        quantise_nope(0)
+        fill_wa(0, 0)
+        fill_wa(0, 1)
+        regroup_wa(0)
+        copy_wa(0, 0)
+        copy_wa(0, 1)
+        transpose_x(0)
+        quantise_wa(0)
+        copy_x(0, 0)
+        copy_x(0, 1)
+        fill_wa(1, 0)
+        fill_wa(1, 1)
+        regroup_wa(1)
+        copy_wa(1, 0)
+        copy_wa(1, 1)
+        quantise_x(0)
+        transpose_x(1)
+        copy_x(1, 0)
+        copy_x(1, 1)
+        quantise_wa(1)
+        fill_wa(2, 0)
+        fill_wa(2, 1)
+        regroup_wa(2)
+        copy_wa(2, 0)
+        copy_wa(2, 1)
+        quantise_x(1)
+        latent_pass(0, 0)
+        fill_wa(3, 0)
+        fill_wa(3, 1)
+        regroup_wa(3)
+        quantise_wa(2)
+        copy_wa(3, 0)
+        copy_wa(3, 1)
+        latent_pass(0, 1)
+        latent_pass(1, 0)
+        latent_pass(1, 1)
+        latent_pass(2, 0)
+        latent_pass(2, 1)
+        quantise_wa(3)
+        spread_gain()
+        latent_pass(3, 0)
+        latent_pass(3, 1)
         rope_passes(0)
+        sum_squares(0)
+        transpose_x(2)
+        sum_squares(1)
+        scale_and_transpose(0)
+        rotate(0)
+        store_rope(0)
+        scale_and_transpose(1)
+        copy_x(2, 0)
+        copy_h(0)
+        regroup_v(0)
+        copy_h(1)
+        copy_x(2, 1)
+        transpose_x(3)
+        quantise_h(0)
+        quantise_v(0)
+        fill_nope(0)
+        product_v(0, 0)
+        copy_x(3, 0)
+        copy_nope(0)
+        store_v(0, 0)
+        copy_x(3, 1)
+        quantise_x(2)
+        quantise_nope(0)
+        quantise_x(3)
+        for c in range(4):
+            latent_pass(c, 2)
+        for c in range(4):
+            latent_pass(c, 3)
+        product_nope(0, 0)
+        rope_passes(1)
+        copy_n(0, 0)
+        sum_squares(2)
+        regroup_v(1)
+        sum_squares(3)
+        rotate(1)
+        store_rope(1)
         scale_and_transpose(2)
         scale_and_transpose(3)
-        for i in range(TILES):
-            copy_h(i)
-        quantise_h(0)
-        second_product(0, 0)
-        rotate(0)
-        spread(0)
-        rope_passes(1)
-        quantise_h(1)
-        store_v(0, 0)
-        store_k(0, 0)
-        regroup_v(1)
-        rotate(1)
-        second_product(0, 1)
         quantise_v(1)
-        spread(1)
+        copy_h(2)
+        copy_h(3)
+        product_v(1, 0)
+        store_v(1, 0)
+        quantise_h(1)
+        product_v(0, 1)
+        product_nope(0, 1)
         store_v(0, 1)
         regroup_nope(1)
-        store_k(0, 1)
+        copy_n(0, 1)
+        product_v(1, 1)
         quantise_nope(1)
-        for g in range(1, GROUPS):
-            for b in range(BATCH):
-                second_product(g, b)
-            if g + 1 < GROUPS:
-                regroup_v(g + 1)
-                regroup_nope(g + 1)
-                quantise_v(g + 1)
-                quantise_nope(g + 1)
-            for b in range(BATCH):
+        store_v(1, 1)
+        product_nope(1, 0)
+        copy_n(1, 0)
+        store_nope(0)
+        product_nope(1, 1)
+        copy_n(1, 1)
+        store_nope(1)
+        for g in (2, 3):
+            regroup_v(g)
+            regroup_nope(g)
+            quantise_v(g)
+            quantise_nope(g)
+            spread(0, g % 2)
+            spread(1, g % 2)
+            for b in range(2):
+                product_v(g, b)
+                product_nope(g, b)
                 store_v(g, b)
-            for b in range(BATCH):
                 store_k(g, b)

@@ -33,10 +33,9 @@ GROUPS = HEADS // GROUP_HEADS
 GROUP_COLS = GROUP_HEADS * HEAD_COLS
 V_COLS = GROUP_HEADS * D_V
 NOPE_COLS = GROUP_HEADS * D_NOPE
-VECTOR_COLS = (384, 256, 256, 256)
-SPLIT_GROUPS = 2
-SPLIT_HEADS = SPLIT_GROUPS * GROUP_HEADS
+VECTOR_COLS = (384, 384, 352, 352)
 FREQS = D_ROPE // 2
+FINE = 8
 RUN = 4
 
 ROUND_MAGIC = 1.5 * 2.0**23
@@ -57,10 +56,10 @@ def tile_multiheadlatentattention_pb_kernel(tc, x, Wkva, kv_a_norm_w, Wkvb, out_
         ctx.enter_context(tc.manual_schedule())
 
         def bank_hold(shape, dtype, name):
-            return psum.tile(shape, dtype, tag="hold", bufs=4, name=name)
+            return psum.tile(shape, dtype, tag="hold", bufs=5, name=name)
 
         def bank_pass(shape, dtype, name):
-            return psum.tile(shape, dtype, tag="pass", bufs=4, name=name)
+            return psum.tile(shape, dtype, tag="pass", bufs=3, name=name)
 
         def quantise(codes, scales, grouped):
             nc.vector.quantize_mx(out=codes.bitcast(FP8X4), scales=scales, in_=grouped)
@@ -104,44 +103,47 @@ def tile_multiheadlatentattention_pb_kernel(tc, x, Wkva, kv_a_norm_w, Wkvb, out_
         )
         zero_col = const.tile([P, 1], F32)
         nc.gpsimd.memset(zero_col[:], 0.0)
-        ident_bf = const.tile([P, P], BF16)
-        make_identity(nc, ident_bf[:])
+        ident_f32 = const.tile([P, P], F32)
+        make_identity(nc, ident_f32[:])
         gain_row = const.tile([P, LATENT], BF16)
         nc.gpsimd.memset(gain_row[:], 0.0)
         load_wa(0)
         load_x(0)
-        load_wa(1)
         load_x(1)
+        load_wa(1)
         nc.sync.dma_start(out=gain_row[0:1, :], in_=kv_a_norm_w.rearrange("(o n) -> o n", o=1))
-        load_wa(2)
-        load_wa(3)
         load_x(2)
+        load_wa(2)
         load_x(3)
+        load_wa(3)
         for g in range(GROUPS):
             load_wb(g)
 
-        ident_f32 = const.tile([P, P], F32)
-        make_identity(nc, ident_f32[:])
+        minus_half = const.tile([P, 1], F32)
+        nc.gpsimd.memset(minus_half[:], -0.5)
         ones = const.tile([P, P], BF16)
         nc.gpsimd.memset(ones[:], 1.0)
 
         warm = const.tile([P, 1], F32)
         nc.scalar.activation(out=warm[:], in_=zero_col[:], func=ACT.Sin)
-        per_pos = const.tile([P, FREQS], F32)
-        nc.vector.memset(per_pos[:], 1.0)
-        for level in range(6):
+        factors = const.tile([P, 2, FINE], F32)
+        nc.vector.memset(factors[:], 1.0)
+        for level in range(3):
             bit = 2**level
-            has_bit = per_pos[:].rearrange("p (a two c) -> p a two c", two=2, c=bit)[:, :, 1, :]
-            nc.vector.tensor_scalar_mul(out=has_bit, in0=has_bit, scalar1=THETA ** (-bit / 64.0))
-        eps_col = const.tile([P, 1], F32)
-        nc.vector.tensor_scalar(out=eps_col[:], in0=zero_col[:], scalar1=1.0, scalar2=EPS, op0=ALU.mult, op1=ALU.add)
-
-        turns = const.tile([P, 2, ROWS, FREQS], F32)
+            for part_of_f, unit in ((0, FINE), (1, 1)):
+                has_bit = factors[:, part_of_f, :].rearrange("p (m two c) -> p m two c", two=2, c=bit)[:, :, 1, :]
+                nc.vector.tensor_scalar_mul(out=has_bit, in0=has_bit, scalar1=THETA ** (-bit * unit / 64.0))
+        per_pos = const.tile([P, FREQS], F32)
         nc.vector.scalar_tensor_tensor(
-            out=turns[:, SIN, :, :], in0=per_pos[:].unsqueeze(1).to_broadcast([P, ROWS, FREQS]),
-            scalar=1.0 / (2.0 * math.pi), in1=pos[:].unsqueeze(2).to_broadcast([P, ROWS, FREQS]),
-            op0=ALU.mult, op1=ALU.mult,
+            out=per_pos[:].rearrange("p (a b) -> p a b", b=FINE),
+            in0=factors[:, 0, :].unsqueeze(2).to_broadcast([P, FINE, FINE]), scalar=1.0 / (2.0 * math.pi),
+            in1=factors[:, 1, :].unsqueeze(1).to_broadcast([P, FINE, FINE]), op0=ALU.mult, op1=ALU.mult,
         )
+        turns = const.tile([P, 2, ROWS, FREQS], F32)
+        for j in range(ROWS):
+            nc.vector.tensor_scalar(
+                out=turns[:, SIN, j, :], in0=per_pos[:], scalar1=pos[:, j : j + 1], scalar2=None, op0=ALU.mult
+            )
         nc.vector.tensor_scalar(
             out=turns[:, COS, :, :], in0=turns[:, SIN, :, :], scalar1=1.0, scalar2=0.25, op0=ALU.mult, op1=ALU.add
         )
@@ -151,16 +153,13 @@ def tile_multiheadlatentattention_pb_kernel(tc, x, Wkva, kv_a_norm_w, Wkvb, out_
         )
         part = const.tile([P, 2, ROWS, FREQS], F32)
         nc.vector.tensor_tensor(out=part[:], in0=turns[:], in1=whole[:], op=ALU.subtract)
-        sin_even = part[:, SIN, :, :].rearrange("p j (m e) -> p (j m) e", e=2)[:, :, 0]
-        nc.vector.tensor_scalar_mul(out=sin_even, in0=sin_even, scalar1=-1.0)
+        sin_pairs = part[:, SIN, :, :].rearrange("p j (m e) -> p (j m) e", e=2)
+        for_read = const.tile([P, ROWS, FREQS], F32)
+        for_read_pairs = for_read[:].rearrange("p j (m e) -> p (j m) e", e=2)
+        nc.vector.tensor_scalar_mul(out=for_read_pairs[:, :, 1], in0=sin_pairs[:, :, 0], scalar1=-1.0)
+        nc.vector.tensor_copy(out=for_read_pairs[:, :, 0], in_=sin_pairs[:, :, 1])
+        nc.vector.tensor_copy(out=part[:, SIN, :, :], in_=for_read[:])
         table = const.tile([P, 2, ROWS, D_ROPE], F32)
-        nc.scalar.activation(
-            out=table[:].rearrange("p s j (h f) -> p (s j) h f", h=2),
-            in_=part[:].rearrange("p s j f -> p (s j) f").unsqueeze(2).to_broadcast([P, 2 * ROWS, 2, FREQS]),
-            func=ACT.Sin, scale=2.0 * math.pi,
-        )
-        warm_norm = const.tile([P, 1], F32)
-        nc.scalar.activation(out=warm_norm[:], in_=eps_col[:], func=ACT.Abs_reciprocal_sqrt)
 
         x_codes = keep.tile([P, TILES, A_PASSES * P], U32, align_bytes=64)
         x_scales = keep.tile([P, TILES, A_PASSES * P], U8, align_bytes=64)
@@ -173,62 +172,56 @@ def tile_multiheadlatentattention_pb_kernel(tc, x, Wkva, kv_a_norm_w, Wkvb, out_
         wn_codes = keep.tile([P, GROUPS, NOPE_COLS], U32, align_bytes=64)
         wn_scales = keep.tile([P, GROUPS, NOPE_COLS], U8, align_bytes=64)
         mean_sq = const.tile([P, TILES], F32)
+        mean_eps = const.tile([P, TILES], F32)
         rstd = const.tile([P, TILES], F32)
         gain = const.tile([P, LATENT], F32)
         h_grouped = keep.tile([P, TILES, P, PACK], BF16, align_bytes=64)
 
         wa_grouped = {}
-        wa_ps = {}
         xT_ps = {}
         x_grouped = {}
+        gain_ps = {}
         latent_ps = {}
         rope_ps = {}
+        h_tiles = {}
         hT_ps = {}
-        wn_ps = {}
         wv_grouped = {}
         wn_grouped = {}
         rotated = {}
         v_ps = {}
         nope_ps = {}
         k_tiles = {}
-        nope_tiles = {}
-        for b in range(BATCH):
-            nope_tiles[b] = keep.tile([P, SPLIT_HEADS, ROWS, D_NOPE], F32, name="nope_tile%d" % b)
+        v_tiles = {}
 
-        def interleave(out, rhs):
-            for t2 in range(PACK // 2):
-                pair = slice(2 * t2, 2 * t2 + 2)
-                nc.tensor.matmul(
-                    out=out.rearrange("p n t -> p t n")[:, pair, :], lhsT=ident_bf[:], rhs=rhs[:, pair, :],
-                    start=True, stop=True,
-                )
+        def sin_table():
+            nc.scalar.activation(
+                out=table[:].rearrange("p s j (h f) -> p (s j) h f", h=2),
+                in_=part[:].rearrange("p s j f -> p (s j) f").unsqueeze(2).to_broadcast([P, 2 * ROWS, 2, FREQS]),
+                func=ACT.Sin, scale=2.0 * math.pi,
+            )
 
-        def psum_cols(c, half):
-            width = (A_COLS - VECTOR_COLS[c]) // 2
-            first = VECTOR_COLS[c] + half * width
-            return slice(first, first + width)
-
-        def fill_wa(c, half):
-            cols = psum_cols(c, half)
-            wa_ps[(c, half)] = bank_pass([P, cols.stop - cols.start, PACK], BF16, "wa_ps%d%d" % (c, half))
-            interleave(wa_ps[(c, half)][:], wa_raw[c][:, :, cols])
+        def interleave(copy, out, rows):
+            copy(out=out.rearrange("p (c i) t -> p c t i", i=RUN), in_=rows.rearrange("p t (c i) -> p c t i", i=RUN))
 
         def regroup_wa(c):
             wa_grouped[c] = stage.tile([P, A_COLS, PACK], BF16, align_bytes=64, name="wa_grouped%d" % c, tag="wa_grouped")
-            nc.vector.tensor_copy(
-                out=wa_grouped[c][:, 0 : VECTOR_COLS[c], :].rearrange("p (c i) t -> p c t i", i=RUN),
-                in_=wa_raw[c][:, :, 0 : VECTOR_COLS[c]].rearrange("p t (c i) -> p c t i", i=RUN),
+            cols = slice(0, VECTOR_COLS[c])
+            interleave(nc.vector.tensor_copy, wa_grouped[c][:, cols, :], wa_raw[c][:, :, cols])
+
+        def copy_wa(c):
+            cols = slice(VECTOR_COLS[c], A_COLS)
+            interleave(nc.scalar.copy, wa_grouped[c][:, cols, :], wa_raw[c][:, :, cols])
+
+        def quantise_wa(c, cols):
+            quantise(
+                wa_codes[:, c, cols], wa_scales[:, c, cols], wa_grouped[c][:, cols, :].rearrange("p n t -> p (n t)")
             )
 
-        def copy_wa(c, half):
-            nc.scalar.copy(out=wa_grouped[c][:, psum_cols(c, half), :], in_=wa_ps[(c, half)][:])
+        def quantise_latent(c):
+            quantise_wa(c, slice(0, LATENT))
 
-        def quantise_wa(c):
-            for cols in (slice(0, LATENT), slice(LATENT, A_COLS)):
-                quantise(
-                    wa_codes[:, c, cols], wa_scales[:, c, cols],
-                    wa_grouped[c][:, cols, :].rearrange("p n t -> p (n t)"),
-                )
+        def quantise_rope(c):
+            quantise_wa(c, slice(LATENT, A_COLS))
 
         def transpose_x(i):
             x_words = x_raw[i][:].bitcast(F32)
@@ -253,10 +246,12 @@ def tile_multiheadlatentattention_pb_kernel(tc, x, Wkva, kv_a_norm_w, Wkvb, out_
         def quantise_x(i):
             quantise(x_codes[:, i, :], x_scales[:, i, :], x_grouped[i][:])
 
-        def spread_gain():
-            gain_ps = bank_pass([P, LATENT], F32, "gain_ps")
-            nc.tensor.matmul(out=gain_ps[:], lhsT=ones[:], rhs=gain_row[:], start=True, stop=True)
-            nc.scalar.copy(out=gain[:], in_=gain_ps[:])
+        def gain_product():
+            gain_ps["all"] = bank_pass([P, LATENT], F32, "gain_ps")
+            nc.tensor.matmul(out=gain_ps["all"][:], lhsT=ones[:], rhs=gain_row[:], start=True, stop=True)
+
+        def gain_copy():
+            nc.scalar.copy(out=gain[:], in_=gain_ps["all"][:])
 
         def latent_pass(c, i):
             if c == 0:
@@ -286,16 +281,19 @@ def tile_multiheadlatentattention_pb_kernel(tc, x, Wkva, kv_a_norm_w, Wkvb, out_
                 out=squares[:], in_=latent_ps[i][:], func=ACT.Square, scale=1.0 / math.sqrt(LATENT),
                 accum_out=mean_sq[:, col],
             )
-            nc.scalar.activation(
-                out=rstd[:, col], in_=mean_sq[:, col], func=ACT.Abs_reciprocal_sqrt, bias=eps_col[:], scale=1.0
+            nc.gpsimd.tensor_scalar(
+                out=mean_eps[:, col], in0=mean_sq[:, col], scalar1=1.0, scalar2=EPS, op0=ALU.mult, op1=ALU.add
+            )
+            nc.gpsimd.tensor_tensor(out=rstd[:, col], in0=mean_eps[:, col], in1=minus_half[:], op=ALU.pow)
+
+        def scale(i):
+            h_tiles[i] = per_tile.tile([P, LATENT], BF16, name="h%d" % i, tag="h")
+            nc.vector.scalar_tensor_tensor(
+                out=h_tiles[i][:], in0=latent_ps[i][:], scalar=rstd[:, i : i + 1], in1=gain[:], op0=ALU.mult, op1=ALU.mult
             )
 
-        def scale_and_transpose(i):
-            h = per_tile.tile([P, LATENT], BF16)
-            nc.vector.scalar_tensor_tensor(
-                out=h[:], in0=latent_ps[i][:], scalar=rstd[:, i : i + 1], in1=gain[:], op0=ALU.mult, op1=ALU.mult
-            )
-            h_words = h[:].bitcast(F32)
+        def transpose_h(i):
+            h_words = h_tiles[i][:].bitcast(F32)
             hT_ps[i] = bank_pass([P, 2, P], F32, "hT_ps%d" % i)
             for u in range(2):
                 nc.tensor.transpose(hT_ps[i][:, u, :], h_words[:, u : 2 * P : 2], ident_f32[:])
@@ -313,28 +311,10 @@ def tile_multiheadlatentattention_pb_kernel(tc, x, Wkva, kv_a_norm_w, Wkvb, out_
                 h_grouped[:, b * ROWS : (b + 1) * ROWS, :, :].rearrange("p i r t -> p (i r t)"),
             )
 
-        def fill_nope(g):
-            wn_ps[g] = bank_pass([P, NOPE_COLS, PACK], BF16, "wn_ps%d" % g)
-            by_head = wb_raw[g][:].rearrange("p t (h f) -> p t h f", f=HEAD_COLS)
-            for t2 in range(PACK // 2):
-                for h2 in range(2):
-                    pair = slice(2 * t2, 2 * t2 + 2)
-                    nc.tensor.matmul(
-                        out=wn_ps[g][:].rearrange("p (h f) t -> p t h f", f=D_NOPE)[:, pair, 2 * h2 : 2 * h2 + 2, :],
-                        lhsT=ident_bf[:], rhs=by_head[:, pair, 2 * h2 : 2 * h2 + 2, 0:D_NOPE], start=True, stop=True,
-                    )
-
-        def group_nope(g):
+        def regroup_nope(g, copy):
             wn_grouped[g] = stage.tile([P, NOPE_COLS, PACK], BF16, align_bytes=64, name="wn_grouped%d" % g, tag="wn_grouped")
-
-        def copy_nope(g):
-            group_nope(g)
-            nc.scalar.copy(out=wn_grouped[g][:], in_=wn_ps[g][:])
-
-        def regroup_nope(g):
-            group_nope(g)
             by_head = wb_raw[g][:].rearrange("p t (h f) -> p h t f", f=HEAD_COLS)
-            nc.vector.tensor_copy(
+            copy(
                 out=wn_grouped[g][:].rearrange("p (h c i) t -> p h c t i", h=GROUP_HEADS, i=RUN),
                 in_=by_head[:, :, :, 0:D_NOPE].rearrange("p h t (c i) -> p h c t i", i=RUN),
             )
@@ -354,19 +334,17 @@ def tile_multiheadlatentattention_pb_kernel(tc, x, Wkva, kv_a_norm_w, Wkvb, out_
             quantise(wn_codes[:, g, :], wn_scales[:, g, :], wn_grouped[g][:].rearrange("p n t -> p (n t)"))
 
         def rotate(b):
-            r_ps = rope_ps[b][:]
             by_cos = stage.tile([P, ROWS, D_ROPE], F32)
-            nc.vector.tensor_tensor(out=by_cos[:], in0=r_ps, in1=table[:, COS, :, :], op=ALU.mult)
+            nc.vector.tensor_tensor(out=by_cos[:], in0=rope_ps[b][:], in1=table[:, COS, :, :], op=ALU.mult)
             by_sin = stage.tile([P, ROWS, D_ROPE], F32)
-            r_pairs = r_ps.rearrange("p j (m e) -> p (j m) e", e=2)
-            sin_pairs = table[:, SIN, :, :].rearrange("p j (m e) -> p (j m) e", e=2)
-            out_pairs = by_sin[:].rearrange("p j (m e) -> p (j m) e", e=2)
-            for e in range(2):
-                nc.vector.tensor_tensor(
-                    out=out_pairs[:, :, e], in0=r_pairs[:, :, 1 - e], in1=sin_pairs[:, :, e], op=ALU.mult
-                )
+            nc.vector.tensor_tensor(out=by_sin[:], in0=rope_ps[b][:], in1=table[:, SIN, :, :], op=ALU.mult)
             rotated[b] = keep.tile([P, ROWS, D_ROPE], F32, name="rotated%d" % b)
-            nc.vector.tensor_tensor(out=rotated[b][:], in0=by_cos[:], in1=by_sin[:], op=ALU.add)
+            nc.vector.tensor_tensor(
+                out=rotated[b][:].rearrange("p j (m e) -> p (j m) e", e=2),
+                in0=by_cos[:].rearrange("p j (m e) -> p (j m) e", e=2),
+                in1=by_sin[:].rearrange("p j (m e) -> p (j m) e", e=2)[:, :, ::-1],
+                op=ALU.add,
+            )
 
         def spread(b, n):
             k_tiles[(b, n)] = keep.tile([P, GROUP_HEADS, ROWS, D_NOPE + D_ROPE], F32, name="k_tile%d%d" % (b, n))
@@ -375,25 +353,22 @@ def tile_multiheadlatentattention_pb_kernel(tc, x, Wkva, kv_a_norm_w, Wkvb, out_
                 in_=rotated[b][:].unsqueeze(1).to_broadcast([P, GROUP_HEADS, ROWS, D_ROPE]),
             )
 
+        def positions(out, j):
+            return out.rearrange("h (p j) f -> p h j f", j=ROWS)[:, :, j, :]
+
         def store_rope(b):
             for j in range(ROWS):
                 nc.sync.dma_start(
-                    out=out_0[b, 0:SPLIT_HEADS].rearrange("h (p j) f -> p h j f", j=ROWS)[:, :, j, D_NOPE:],
-                    in_=rotated[b][:, j, :].unsqueeze(1).to_broadcast([P, SPLIT_HEADS, D_ROPE]),
+                    out=positions(out_0[b], j)[:, :, D_NOPE:],
+                    in_=rotated[b][:, j, :].unsqueeze(1).to_broadcast([P, HEADS, D_ROPE]),
                 )
 
-        def copy_n(g, b):
-            nc.scalar.copy(
-                out=nope_tiles[b][:, g * GROUP_HEADS : (g + 1) * GROUP_HEADS, :, :],
-                in_=nope_ps[(g, b)][:].rearrange("p j (h f) -> p h j f", h=GROUP_HEADS),
-            )
-
-        def store_nope(b):
+        def store_nope(g, b):
+            heads = slice(g * GROUP_HEADS, (g + 1) * GROUP_HEADS)
+            nope_tile = per_tile.tile([P, GROUP_HEADS, ROWS, D_NOPE], F32)
+            nc.scalar.copy(out=nope_tile[:], in_=nope_ps[(g, b)][:].rearrange("p j (h f) -> p h j f", h=GROUP_HEADS))
             for j in range(ROWS):
-                nc.sync.dma_start(
-                    out=out_0[b, 0:SPLIT_HEADS].rearrange("h (p j) f -> p h j f", j=ROWS)[:, :, j, 0:D_NOPE],
-                    in_=nope_tiles[b][:, :, j, :],
-                )
+                nc.sync.dma_start(out=positions(out_0[b, heads], j)[:, :, 0:D_NOPE], in_=nope_tile[:, :, j, :])
 
         def tokens(b, j):
             return slice((b * ROWS + j) * P, (b * ROWS + j + 1) * P)
@@ -416,17 +391,22 @@ def tile_multiheadlatentattention_pb_kernel(tc, x, Wkva, kv_a_norm_w, Wkvb, out_
                     wn_codes[:, g, :], wn_scales[:, g, :], start=True, stop=True,
                 )
 
-        def store_v(g, b):
+        def copy_v(g, b, j, copy):
+            if (g, b) not in v_tiles:
+                v_tiles[(g, b)] = per_tile.tile([P, GROUP_HEADS, ROWS, D_V], F32, name="v_tile%d%d" % (g, b), tag="v_tile")
+            copy(out=v_tiles[(g, b)][:, :, j, :], in_=v_ps[(g, b, j)][:].rearrange("p (h f) -> p h f", h=GROUP_HEADS))
+
+        def send_v(g, b):
             heads = slice(g * GROUP_HEADS, (g + 1) * GROUP_HEADS)
-            v_tile = per_tile.tile([P, GROUP_HEADS, ROWS, D_V], F32)
-            for j in range(ROWS):
-                nc.scalar.copy(
-                    out=v_tile[:, :, j, :], in_=v_ps[(g, b, j)][:].rearrange("p (h f) -> p h f", h=GROUP_HEADS)
-                )
             nc.sync.dma_start(
                 out=out_1[b, heads].rearrange("h (p j) f -> p h (j f)", j=ROWS),
-                in_=v_tile[:].rearrange("p h j f -> p h (j f)"),
+                in_=v_tiles[(g, b)][:].rearrange("p h j f -> p h (j f)"),
             )
+
+        def store_v(g, b):
+            for j in range(ROWS):
+                copy_v(g, b, j, nc.scalar.copy)
+            send_v(g, b)
 
         def store_k(g, b):
             heads = slice(g * GROUP_HEADS, (g + 1) * GROUP_HEADS)
@@ -440,115 +420,117 @@ def tile_multiheadlatentattention_pb_kernel(tc, x, Wkva, kv_a_norm_w, Wkvb, out_
                 in_=k_tile[:].rearrange("p h j f -> p h (j f)"),
             )
 
-        fill_wa(0, 0)
-        fill_wa(0, 1)
         regroup_wa(0)
-        copy_wa(0, 0)
-        copy_wa(0, 1)
+        copy_wa(0)
         transpose_x(0)
-        quantise_wa(0)
         copy_x(0, 0)
         copy_x(0, 1)
-        fill_wa(1, 0)
-        fill_wa(1, 1)
-        regroup_wa(1)
-        copy_wa(1, 0)
-        copy_wa(1, 1)
-        quantise_x(0)
+        quantise_rope(0)
+        quantise_latent(0)
         transpose_x(1)
         copy_x(1, 0)
+        quantise_x(0)
         copy_x(1, 1)
-        quantise_wa(1)
-        fill_wa(2, 0)
-        fill_wa(2, 1)
-        regroup_wa(2)
-        copy_wa(2, 0)
-        copy_wa(2, 1)
+        regroup_wa(1)
+        copy_wa(1)
         quantise_x(1)
+        transpose_x(2)
         latent_pass(0, 0)
-        fill_wa(3, 0)
-        fill_wa(3, 1)
-        regroup_wa(3)
-        quantise_wa(2)
-        copy_wa(3, 0)
-        copy_wa(3, 1)
+        quantise_rope(1)
+        quantise_latent(1)
+        copy_x(2, 0)
+        copy_x(2, 1)
         latent_pass(0, 1)
         latent_pass(1, 0)
+        regroup_wa(2)
+        copy_wa(2)
+        quantise_x(2)
+        transpose_x(3)
+        copy_x(3, 0)
+        copy_x(3, 1)
+        gain_product()
         latent_pass(1, 1)
+        latent_pass(0, 2)
+        latent_pass(1, 2)
+        quantise_rope(2)
+        quantise_latent(2)
+        regroup_wa(3)
+        copy_wa(3)
+        quantise_x(3)
+        quantise_rope(3)
         latent_pass(2, 0)
         latent_pass(2, 1)
-        quantise_wa(3)
-        spread_gain()
+        latent_pass(2, 2)
+        rope_passes(0)
+        quantise_latent(3)
         latent_pass(3, 0)
         latent_pass(3, 1)
-        rope_passes(0)
-        sum_squares(0)
-        transpose_x(2)
-        sum_squares(1)
-        scale_and_transpose(0)
+        sin_table()
+        gain_copy()
         rotate(0)
         store_rope(0)
-        scale_and_transpose(1)
-        copy_x(2, 0)
-        copy_h(0)
         regroup_v(0)
-        copy_h(1)
-        copy_x(2, 1)
-        transpose_x(3)
-        quantise_h(0)
-        quantise_v(0)
-        fill_nope(0)
-        product_v(0, 0)
-        copy_x(3, 0)
-        copy_nope(0)
-        store_v(0, 0)
-        copy_x(3, 1)
-        quantise_x(2)
-        quantise_nope(0)
-        quantise_x(3)
-        for c in range(4):
-            latent_pass(c, 2)
-        for c in range(4):
+        sum_squares(0)
+        sum_squares(1)
+        for c in range(3):
             latent_pass(c, 3)
-        product_nope(0, 0)
+        latent_pass(3, 2)
+        latent_pass(3, 3)
         rope_passes(1)
-        copy_n(0, 0)
+        scale(0)
+        transpose_h(0)
+        regroup_nope(0, nc.scalar.copy)
         sum_squares(2)
-        regroup_v(1)
+        scale(1)
+        transpose_h(1)
+        copy_h(0)
+        quantise_v(0)
+        copy_h(1)
         sum_squares(3)
-        rotate(1)
-        store_rope(1)
-        scale_and_transpose(2)
-        scale_and_transpose(3)
-        quantise_v(1)
+        quantise_h(0)
+        product_v(0, 0)
+        quantise_nope(0)
+        product_nope(0, 0)
+        scale(2)
+        transpose_h(2)
+        copy_v(0, 0, 0, nc.scalar.copy)
+        copy_v(0, 0, 1, nc.vector.tensor_copy)
+        send_v(0, 0)
+        store_nope(0, 0)
+        scale(3)
+        transpose_h(3)
         copy_h(2)
         copy_h(3)
-        product_v(1, 0)
-        store_v(1, 0)
+        regroup_v(1)
         quantise_h(1)
         product_v(0, 1)
+        quantise_v(1)
         product_nope(0, 1)
         store_v(0, 1)
-        regroup_nope(1)
-        copy_n(0, 1)
+        product_v(1, 0)
+        store_v(1, 0)
+        rotate(1)
+        spread(1, 0)
         product_v(1, 1)
-        quantise_nope(1)
         store_v(1, 1)
+        store_k(0, 1)
+        regroup_nope(1, nc.vector.tensor_copy)
+        quantise_nope(1)
+        spread(1, 1)
         product_nope(1, 0)
-        copy_n(1, 0)
-        store_nope(0)
+        store_nope(1, 0)
         product_nope(1, 1)
-        copy_n(1, 1)
-        store_nope(1)
-        for g in (2, 3):
+        store_k(1, 1)
+        for g in range(2, 4):
             regroup_v(g)
-            regroup_nope(g)
+            regroup_nope(g, nc.vector.tensor_copy)
             quantise_v(g)
             quantise_nope(g)
-            spread(0, g % 2)
-            spread(1, g % 2)
-            for b in range(2):
-                product_v(g, b)
-                product_nope(g, b)
-                store_v(g, b)
-                store_k(g, b)
+            product_v(g, 0)
+            product_nope(g, 0)
+            store_v(g, 0)
+            store_nope(g, 0)
+            product_v(g, 1)
+            product_nope(g, 1)
+            store_v(g, 1)
+            store_k(g, 1)

@@ -38,6 +38,9 @@ FREQS = D_ROPE // 2
 FINE = 8
 RUN = 4
 
+FIRST_HEADS, LAST_HEADS = slice(0, GROUP_HEADS // 2), slice(GROUP_HEADS // 2, GROUP_HEADS)
+ALL_HEADS = slice(0, GROUP_HEADS)
+
 ROUND_MAGIC = 1.5 * 2.0**23
 COS, SIN = 0, 1
 
@@ -243,8 +246,11 @@ def tile_multiheadlatentattention_pb_kernel(tc, x, Wkva, kv_a_norm_w, Wkvb, out_
                 in_=xT_ps[(i, half)][:].rearrange("p c u r -> p c r u"),
             )
 
-        def quantise_x(i):
-            quantise(x_codes[:, i, :], x_scales[:, i, :], x_grouped[i][:])
+        def quantise_x(i, halves=(0, 2)):
+            words = slice(halves[0] * 2 * P, halves[1] * 2 * P)
+            quantise(
+                x_codes[:, i, words], x_scales[:, i, words], x_grouped[i][:, words.start * PACK : words.stop * PACK]
+            )
 
         def gain_product():
             gain_ps["all"] = bank_pass([P, LATENT], F32, "gain_ps")
@@ -304,12 +310,9 @@ def tile_multiheadlatentattention_pb_kernel(tc, x, Wkva, kv_a_norm_w, Wkvb, out_
                 in_=hT_ps[i][:].rearrange("p u r -> p r u"),
             )
 
-        def quantise_h(b):
-            toks = slice(b * ROWS * P, (b + 1) * ROWS * P)
-            quantise(
-                h_codes[:, toks], h_scales[:, toks],
-                h_grouped[:, b * ROWS : (b + 1) * ROWS, :, :].rearrange("p i r t -> p (i r t)"),
-            )
+        def quantise_h(i):
+            toks = slice(i * P, (i + 1) * P)
+            quantise(h_codes[:, toks], h_scales[:, toks], h_grouped[:, i, :, :].rearrange("p r t -> p (r t)"))
 
         def regroup_nope(g, copy):
             wn_grouped[g] = stage.tile([P, NOPE_COLS, PACK], BF16, align_bytes=64, name="wn_grouped%d" % g, tag="wn_grouped")
@@ -319,12 +322,13 @@ def tile_multiheadlatentattention_pb_kernel(tc, x, Wkva, kv_a_norm_w, Wkvb, out_
                 in_=by_head[:, :, :, 0:D_NOPE].rearrange("p h t (c i) -> p h c t i", i=RUN),
             )
 
-        def regroup_v(g):
-            wv_grouped[g] = stage.tile([P, V_COLS * PACK], BF16, align_bytes=64, name="wv_grouped%d" % g, tag="wv_grouped")
+        def regroup_v(g, heads, copy):
+            if g not in wv_grouped:
+                wv_grouped[g] = stage.tile([P, V_COLS * PACK], BF16, align_bytes=64, name="wv_grouped%d" % g, tag="wv_grouped")
             by_head = wb_raw[g][:].rearrange("p t (h f) -> p h t f", f=HEAD_COLS)
-            nc.vector.tensor_copy(
-                out=wv_grouped[g][:].rearrange("p (h c i t) -> p h c t i", h=GROUP_HEADS, i=RUN, t=PACK),
-                in_=by_head[:, :, :, D_NOPE:].rearrange("p h t (c i) -> p h c t i", i=RUN),
+            copy(
+                out=wv_grouped[g][:].rearrange("p (h c i t) -> p h c t i", h=GROUP_HEADS, i=RUN, t=PACK)[:, heads],
+                in_=by_head[:, heads, :, D_NOPE:].rearrange("p h t (c i) -> p h c t i", i=RUN),
             )
 
         def quantise_v(g):
@@ -373,14 +377,13 @@ def tile_multiheadlatentattention_pb_kernel(tc, x, Wkva, kv_a_norm_w, Wkvb, out_
         def tokens(b, j):
             return slice((b * ROWS + j) * P, (b * ROWS + j + 1) * P)
 
-        def product_v(g, b):
-            for j in range(ROWS):
-                toks = tokens(b, j)
-                v_ps[(g, b, j)] = bank_pass([P, V_COLS], F32, "v_ps%d%d%d" % (g, b, j))
-                mx_pass(
-                    v_ps[(g, b, j)][:], h_codes[:, toks], h_scales[:, toks],
-                    wv_codes[:, g, :], wv_scales[:, g, :], start=True, stop=True,
-                )
+        def product_v(g, b, j):
+            toks = tokens(b, j)
+            v_ps[(g, b, j)] = bank_pass([P, V_COLS], F32, "v_ps%d%d%d" % (g, b, j))
+            mx_pass(
+                v_ps[(g, b, j)][:], h_codes[:, toks], h_scales[:, toks],
+                wv_codes[:, g, :], wv_scales[:, g, :], start=True, stop=True,
+            )
 
         def product_nope(g, b):
             nope_ps[(g, b)] = bank_hold([P, ROWS, NOPE_COLS], F32, "nope_ps%d%d" % (g, b))
@@ -391,10 +394,12 @@ def tile_multiheadlatentattention_pb_kernel(tc, x, Wkva, kv_a_norm_w, Wkvb, out_
                     wn_codes[:, g, :], wn_scales[:, g, :], start=True, stop=True,
                 )
 
-        def copy_v(g, b, j, copy):
+        def copy_v(g, b, j):
             if (g, b) not in v_tiles:
                 v_tiles[(g, b)] = per_tile.tile([P, GROUP_HEADS, ROWS, D_V], F32, name="v_tile%d%d" % (g, b), tag="v_tile")
-            copy(out=v_tiles[(g, b)][:, :, j, :], in_=v_ps[(g, b, j)][:].rearrange("p (h f) -> p h f", h=GROUP_HEADS))
+            nc.scalar.copy(
+                out=v_tiles[(g, b)][:, :, j, :], in_=v_ps[(g, b, j)][:].rearrange("p (h f) -> p h f", h=GROUP_HEADS)
+            )
 
         def send_v(g, b):
             heads = slice(g * GROUP_HEADS, (g + 1) * GROUP_HEADS)
@@ -405,7 +410,7 @@ def tile_multiheadlatentattention_pb_kernel(tc, x, Wkva, kv_a_norm_w, Wkvb, out_
 
         def store_v(g, b):
             for j in range(ROWS):
-                copy_v(g, b, j, nc.scalar.copy)
+                copy_v(g, b, j)
             send_v(g, b)
 
         def store_k(g, b):
@@ -422,6 +427,7 @@ def tile_multiheadlatentattention_pb_kernel(tc, x, Wkva, kv_a_norm_w, Wkvb, out_
 
         regroup_wa(0)
         copy_wa(0)
+        sin_table()
         transpose_x(0)
         copy_x(0, 0)
         copy_x(0, 1)
@@ -429,7 +435,8 @@ def tile_multiheadlatentattention_pb_kernel(tc, x, Wkva, kv_a_norm_w, Wkvb, out_
         quantise_latent(0)
         transpose_x(1)
         copy_x(1, 0)
-        quantise_x(0)
+        quantise_x(0, (0, 1))
+        quantise_x(0, (1, 2))
         copy_x(1, 1)
         regroup_wa(1)
         copy_wa(1)
@@ -465,12 +472,12 @@ def tile_multiheadlatentattention_pb_kernel(tc, x, Wkva, kv_a_norm_w, Wkvb, out_
         quantise_latent(3)
         latent_pass(3, 0)
         latent_pass(3, 1)
-        sin_table()
         gain_copy()
         rotate(0)
         store_rope(0)
-        regroup_v(0)
+        regroup_nope(0, nc.scalar.copy)
         sum_squares(0)
+        regroup_v(0, LAST_HEADS, nc.vector.tensor_copy)
         sum_squares(1)
         for c in range(3):
             latent_pass(c, 3)
@@ -478,40 +485,47 @@ def tile_multiheadlatentattention_pb_kernel(tc, x, Wkva, kv_a_norm_w, Wkvb, out_
         latent_pass(3, 3)
         rope_passes(1)
         scale(0)
+        regroup_v(0, FIRST_HEADS, nc.scalar.copy)
         transpose_h(0)
-        regroup_nope(0, nc.scalar.copy)
-        sum_squares(2)
         scale(1)
+        sum_squares(2)
         transpose_h(1)
         copy_h(0)
         quantise_v(0)
-        copy_h(1)
-        sum_squares(3)
         quantise_h(0)
-        product_v(0, 0)
+        product_v(0, 0, 0)
+        sum_squares(3)
+        copy_h(1)
+        copy_v(0, 0, 0)
+        quantise_h(1)
+        product_v(0, 0, 1)
         quantise_nope(0)
+        copy_v(0, 0, 1)
+        send_v(0, 0)
         product_nope(0, 0)
         scale(2)
         transpose_h(2)
-        copy_v(0, 0, 0, nc.scalar.copy)
-        copy_v(0, 0, 1, nc.vector.tensor_copy)
-        send_v(0, 0)
         store_nope(0, 0)
         scale(3)
         transpose_h(3)
         copy_h(2)
         copy_h(3)
-        regroup_v(1)
-        quantise_h(1)
-        product_v(0, 1)
+        regroup_v(1, FIRST_HEADS, nc.vector.tensor_copy)
+        quantise_h(2)
+        quantise_h(3)
+        product_v(0, 1, 0)
+        product_v(0, 1, 1)
+        regroup_v(1, LAST_HEADS, nc.vector.tensor_copy)
         quantise_v(1)
         product_nope(0, 1)
         store_v(0, 1)
-        product_v(1, 0)
+        product_v(1, 0, 0)
+        product_v(1, 0, 1)
         store_v(1, 0)
         rotate(1)
         spread(1, 0)
-        product_v(1, 1)
+        product_v(1, 1, 0)
+        product_v(1, 1, 1)
         store_v(1, 1)
         store_k(0, 1)
         regroup_nope(1, nc.vector.tensor_copy)
@@ -522,15 +536,17 @@ def tile_multiheadlatentattention_pb_kernel(tc, x, Wkva, kv_a_norm_w, Wkvb, out_
         product_nope(1, 1)
         store_k(1, 1)
         for g in range(2, 4):
-            regroup_v(g)
+            regroup_v(g, ALL_HEADS, nc.vector.tensor_copy)
             regroup_nope(g, nc.vector.tensor_copy)
             quantise_v(g)
             quantise_nope(g)
-            product_v(g, 0)
+            product_v(g, 0, 0)
+            product_v(g, 0, 1)
             product_nope(g, 0)
             store_v(g, 0)
             store_nope(g, 0)
-            product_v(g, 1)
+            product_v(g, 1, 0)
+            product_v(g, 1, 1)
             product_nope(g, 1)
             store_v(g, 1)
             store_k(g, 1)

@@ -38,6 +38,7 @@ FREQS = D_ROPE // 2
 FINE = 8
 RUN = 4
 
+K_RUN = D_NOPE + D_ROPE + D_NOPE
 FIRST_HEADS, LAST_HEADS = slice(0, GROUP_HEADS // 2), slice(GROUP_HEADS // 2, GROUP_HEADS)
 ALL_HEADS = slice(0, GROUP_HEADS)
 
@@ -190,6 +191,8 @@ def tile_multiheadlatentattention_pb_kernel(tc, x, Wkva, kv_a_norm_w, Wkvb, out_
         hT_ps = {}
         wv_grouped = {}
         wn_grouped = {}
+        by_cos = {}
+        by_sin = {}
         rotated = {}
         v_ps = {}
         nope_ps = {}
@@ -268,14 +271,14 @@ def tile_multiheadlatentattention_pb_kernel(tc, x, Wkva, kv_a_norm_w, Wkvb, out_
                 wa_codes[:, c, 0:LATENT], wa_scales[:, c, 0:LATENT], start=(c == 0), stop=(c == A_PASSES - 1),
             )
 
-        def rope_passes(b):
-            rope_ps[b] = bank_hold([P, ROWS, D_ROPE], F32, "rope_ps%d" % b)
-            for j in range(ROWS):
+        def rope_passes(j):
+            rope_ps[j] = bank_hold([P, BATCH, D_ROPE], F32, "rope_ps%d" % j)
+            for b in range(BATCH):
                 i = b * ROWS + j
                 for c in range(A_PASSES):
                     toks = slice(c * P, (c + 1) * P)
                     mx_pass(
-                        rope_ps[b][:, j, :], x_codes[:, i, toks], x_scales[:, i, toks],
+                        rope_ps[j][:, b, :], x_codes[:, i, toks], x_scales[:, i, toks],
                         wa_codes[:, c, LATENT:A_COLS], wa_scales[:, c, LATENT:A_COLS],
                         start=(c == 0), stop=(c == A_PASSES - 1),
                     )
@@ -337,42 +340,40 @@ def tile_multiheadlatentattention_pb_kernel(tc, x, Wkva, kv_a_norm_w, Wkvb, out_
         def quantise_nope(g):
             quantise(wn_codes[:, g, :], wn_scales[:, g, :], wn_grouped[g][:].rearrange("p n t -> p (n t)"))
 
-        def rotate(b):
-            by_cos = stage.tile([P, ROWS, D_ROPE], F32)
-            nc.vector.tensor_tensor(out=by_cos[:], in0=rope_ps[b][:], in1=table[:, COS, :, :], op=ALU.mult)
-            by_sin = stage.tile([P, ROWS, D_ROPE], F32)
-            nc.vector.tensor_tensor(out=by_sin[:], in0=rope_ps[b][:], in1=table[:, SIN, :, :], op=ALU.mult)
-            rotated[b] = keep.tile([P, ROWS, D_ROPE], F32, name="rotated%d" % b)
+        def times_table(j, which, products):
+            products[j] = stage.tile([P, BATCH, D_ROPE], F32, name="product%d%d" % (which, j), tag="product%d" % which)
             nc.vector.tensor_tensor(
-                out=rotated[b][:].rearrange("p j (m e) -> p (j m) e", e=2),
-                in0=by_cos[:].rearrange("p j (m e) -> p (j m) e", e=2),
-                in1=by_sin[:].rearrange("p j (m e) -> p (j m) e", e=2)[:, :, ::-1],
+                out=products[j][:], in0=rope_ps[j][:],
+                in1=table[:, which, j, :].unsqueeze(1).to_broadcast([P, BATCH, D_ROPE]), op=ALU.mult,
+            )
+
+        def rotate_cos(j):
+            times_table(j, COS, by_cos)
+
+        def rotate_sin(j):
+            times_table(j, SIN, by_sin)
+
+        def rotate_add(j):
+            rotated[j] = keep.tile([P, BATCH, D_ROPE], F32, name="rotated%d" % j)
+            nc.vector.tensor_tensor(
+                out=rotated[j][:].rearrange("p b (m e) -> p (b m) e", e=2),
+                in0=by_cos[j][:].rearrange("p b (m e) -> p (b m) e", e=2),
+                in1=by_sin[j][:].rearrange("p b (m e) -> p (b m) e", e=2)[:, :, ::-1],
                 op=ALU.add,
             )
 
         def spread(b, n):
             k_tiles[(b, n)] = keep.tile([P, GROUP_HEADS, ROWS, D_NOPE + D_ROPE], F32, name="k_tile%d%d" % (b, n))
             nc.vector.tensor_copy(
-                out=k_tiles[(b, n)][:, :, :, D_NOPE:],
-                in_=rotated[b][:].unsqueeze(1).to_broadcast([P, GROUP_HEADS, ROWS, D_ROPE]),
+                out=k_tiles[(b, n)][:, :, 0, D_NOPE:],
+                in_=rotated[0][:, b, :].unsqueeze(1).to_broadcast([P, GROUP_HEADS, D_ROPE]),
             )
 
-        def positions(out, j):
-            return out.rearrange("h (p j) f -> p h j f", j=ROWS)[:, :, j, :]
-
-        def store_rope(b):
-            for j in range(ROWS):
-                nc.sync.dma_start(
-                    out=positions(out_0[b], j)[:, :, D_NOPE:],
-                    in_=rotated[b][:, j, :].unsqueeze(1).to_broadcast([P, HEADS, D_ROPE]),
-                )
-
-        def store_nope(g, b):
-            heads = slice(g * GROUP_HEADS, (g + 1) * GROUP_HEADS)
-            nope_tile = per_tile.tile([P, GROUP_HEADS, ROWS, D_NOPE], F32)
-            nc.scalar.copy(out=nope_tile[:], in_=nope_ps[(g, b)][:].rearrange("p j (h f) -> p h j f", h=GROUP_HEADS))
-            for j in range(ROWS):
-                nc.sync.dma_start(out=positions(out_0[b, heads], j)[:, :, 0:D_NOPE], in_=nope_tile[:, :, j, :])
+        def store_odd_rope(b):
+            nc.sync.dma_start(
+                out=out_0[b].rearrange("h (p j) f -> p h j f", j=ROWS)[:, :, 1, D_NOPE:],
+                in_=rotated[1][:, b, :].unsqueeze(1).to_broadcast([P, HEADS, D_ROPE]),
+            )
 
         def tokens(b, j):
             return slice((b * ROWS + j) * P, (b * ROWS + j + 1) * P)
@@ -421,8 +422,8 @@ def tile_multiheadlatentattention_pb_kernel(tc, x, Wkva, kv_a_norm_w, Wkvb, out_
                 in_=nope_ps[(g, b)][:].rearrange("p j (h f) -> p h j f", h=GROUP_HEADS),
             )
             nc.sync.dma_start(
-                out=out_0[b, heads].rearrange("h (p j) f -> p h (j f)", j=ROWS),
-                in_=k_tile[:].rearrange("p h j f -> p h (j f)"),
+                out=out_0[b, heads].rearrange("h (p j) f -> p h (j f)", j=ROWS)[:, :, 0:K_RUN],
+                in_=k_tile[:].rearrange("p h j f -> p h (j f)")[:, :, 0:K_RUN],
             )
 
         regroup_wa(0)
@@ -468,13 +469,16 @@ def tile_multiheadlatentattention_pb_kernel(tc, x, Wkva, kv_a_norm_w, Wkvb, out_
         latent_pass(2, 0)
         latent_pass(2, 1)
         latent_pass(2, 2)
-        rope_passes(0)
+        rope_passes(1)
         quantise_latent(3)
         latent_pass(3, 0)
         latent_pass(3, 1)
         gain_copy()
-        rotate(0)
-        store_rope(0)
+        rotate_cos(1)
+        rotate_sin(1)
+        rotate_add(1)
+        store_odd_rope(0)
+        store_odd_rope(1)
         regroup_nope(0, nc.scalar.copy)
         sum_squares(0)
         regroup_v(0, LAST_HEADS, nc.vector.tensor_copy)
@@ -483,10 +487,11 @@ def tile_multiheadlatentattention_pb_kernel(tc, x, Wkva, kv_a_norm_w, Wkvb, out_
             latent_pass(c, 3)
         latent_pass(3, 2)
         latent_pass(3, 3)
-        rope_passes(1)
+        rope_passes(0)
         scale(0)
         regroup_v(0, FIRST_HEADS, nc.scalar.copy)
         transpose_h(0)
+        rotate_cos(0)
         scale(1)
         sum_squares(2)
         transpose_h(1)
@@ -495,6 +500,7 @@ def tile_multiheadlatentattention_pb_kernel(tc, x, Wkva, kv_a_norm_w, Wkvb, out_
         quantise_h(0)
         product_v(0, 0, 0)
         sum_squares(3)
+        rotate_sin(0)
         copy_h(1)
         copy_v(0, 0, 0)
         quantise_h(1)
@@ -505,34 +511,36 @@ def tile_multiheadlatentattention_pb_kernel(tc, x, Wkva, kv_a_norm_w, Wkvb, out_
         product_nope(0, 0)
         scale(2)
         transpose_h(2)
-        store_nope(0, 0)
         scale(3)
         transpose_h(3)
         copy_h(2)
+        rotate_add(0)
+        spread(0, 0)
         copy_h(3)
-        regroup_v(1, FIRST_HEADS, nc.vector.tensor_copy)
+        store_k(0, 0)
         quantise_h(2)
         quantise_h(3)
         product_v(0, 1, 0)
         product_v(0, 1, 1)
+        spread(1, 0)
+        store_v(0, 1)
+        product_nope(0, 1)
+        regroup_v(1, FIRST_HEADS, nc.vector.tensor_copy)
         regroup_v(1, LAST_HEADS, nc.vector.tensor_copy)
         quantise_v(1)
-        product_nope(0, 1)
-        store_v(0, 1)
+        store_k(0, 1)
         product_v(1, 0, 0)
         product_v(1, 0, 1)
         store_v(1, 0)
-        rotate(1)
-        spread(1, 0)
         product_v(1, 1, 0)
         product_v(1, 1, 1)
+        spread(0, 1)
         store_v(1, 1)
-        store_k(0, 1)
         regroup_nope(1, nc.vector.tensor_copy)
         quantise_nope(1)
         spread(1, 1)
         product_nope(1, 0)
-        store_nope(1, 0)
+        store_k(1, 0)
         product_nope(1, 1)
         store_k(1, 1)
         for g in range(2, 4):
@@ -540,13 +548,9 @@ def tile_multiheadlatentattention_pb_kernel(tc, x, Wkva, kv_a_norm_w, Wkvb, out_
             regroup_nope(g, nc.vector.tensor_copy)
             quantise_v(g)
             quantise_nope(g)
-            product_v(g, 0, 0)
-            product_v(g, 0, 1)
-            product_nope(g, 0)
-            store_v(g, 0)
-            store_nope(g, 0)
-            product_v(g, 1, 0)
-            product_v(g, 1, 1)
-            product_nope(g, 1)
-            store_v(g, 1)
-            store_k(g, 1)
+            for b in range(2):
+                product_v(g, b, 0)
+                product_v(g, b, 1)
+                product_nope(g, b)
+                store_v(g, b)
+                store_k(g, b)

@@ -33,7 +33,7 @@ GROUPS = HEADS // GROUP_HEADS
 GROUP_COLS = GROUP_HEADS * HEAD_COLS
 V_COLS = GROUP_HEADS * D_V
 NOPE_COLS = GROUP_HEADS * D_NOPE
-VECTOR_COLS = (384, 384, 352, 352)
+VECTOR_COLS = (576, 384, 352, 352)
 FREQS = D_ROPE // 2
 FINE = 8
 RUN = 4
@@ -143,26 +143,18 @@ def tile_multiheadlatentattention_pb_kernel(tc, x, Wkva, kv_a_norm_w, Wkvb, out_
             in0=factors[:, 0, :].unsqueeze(2).to_broadcast([P, FINE, FINE]), scalar=1.0 / (2.0 * math.pi),
             in1=factors[:, 1, :].unsqueeze(1).to_broadcast([P, FINE, FINE]), op0=ALU.mult, op1=ALU.mult,
         )
-        turns = const.tile([P, 2, ROWS, FREQS], F32)
+        turns = const.tile([P, ROWS, FREQS], F32)
         for j in range(ROWS):
             nc.vector.tensor_scalar(
-                out=turns[:, SIN, j, :], in0=per_pos[:], scalar1=pos[:, j : j + 1], scalar2=None, op0=ALU.mult
+                out=turns[:, j, :], in0=per_pos[:], scalar1=pos[:, j : j + 1], scalar2=None, op0=ALU.mult
             )
-        nc.vector.tensor_scalar(
-            out=turns[:, COS, :, :], in0=turns[:, SIN, :, :], scalar1=1.0, scalar2=0.25, op0=ALU.mult, op1=ALU.add
-        )
-        whole = const.tile([P, 2, ROWS, FREQS], F32)
+        whole = const.tile([P, ROWS, FREQS], F32)
         nc.vector.tensor_scalar(
             out=whole[:], in0=turns[:], scalar1=ROUND_MAGIC, scalar2=ROUND_MAGIC, op0=ALU.add, op1=ALU.subtract
         )
-        part = const.tile([P, 2, ROWS, FREQS], F32)
+        part = const.tile([P, ROWS, FREQS], F32)
         nc.vector.tensor_tensor(out=part[:], in0=turns[:], in1=whole[:], op=ALU.subtract)
-        sin_pairs = part[:, SIN, :, :].rearrange("p j (m e) -> p (j m) e", e=2)
-        for_read = const.tile([P, ROWS, FREQS], F32)
-        for_read_pairs = for_read[:].rearrange("p j (m e) -> p (j m) e", e=2)
-        nc.vector.tensor_scalar_mul(out=for_read_pairs[:, :, 1], in0=sin_pairs[:, :, 0], scalar1=-1.0)
-        nc.vector.tensor_copy(out=for_read_pairs[:, :, 0], in_=sin_pairs[:, :, 1])
-        nc.vector.tensor_copy(out=part[:, SIN, :, :], in_=for_read[:])
+        size = const.tile([P, ROWS, FREQS], F32)
         table = const.tile([P, 2, ROWS, D_ROPE], F32)
 
         x_codes = keep.tile([P, TILES, A_PASSES * P], U32, align_bytes=64)
@@ -200,11 +192,19 @@ def tile_multiheadlatentattention_pb_kernel(tc, x, Wkva, kv_a_norm_w, Wkvb, out_
         v_tiles = {}
 
         def sin_table():
+            nc.scalar.activation(out=size[:], in_=part[:], func=ACT.Abs)
             nc.scalar.activation(
-                out=table[:].rearrange("p s j (h f) -> p (s j) h f", h=2),
-                in_=part[:].rearrange("p s j f -> p (s j) f").unsqueeze(2).to_broadcast([P, 2 * ROWS, 2, FREQS]),
-                func=ACT.Sin, scale=2.0 * math.pi,
+                out=table[:, COS, :, :].rearrange("p j (h f) -> p j h f", h=2),
+                in_=size[:].unsqueeze(2).to_broadcast([P, ROWS, 2, FREQS]),
+                func=ACT.Sin, scale=-2.0 * math.pi, bias=math.pi / 2.0,
             )
+            for e, sign in ((0, 1.0), (1, -1.0)):
+                nc.scalar.activation(
+                    out=table[:, SIN, :, :].rearrange("p j (h m e) -> p j h m e", h=2, e=2)[:, :, :, :, e],
+                    in_=part[:].rearrange("p j (m e) -> p j m e", e=2)[:, :, :, 1 - e]
+                    .unsqueeze(2).to_broadcast([P, ROWS, 2, FREQS // 2]),
+                    func=ACT.Sin, scale=sign * 2.0 * math.pi,
+                )
 
         def interleave(copy, out, rows):
             copy(out=out.rearrange("p (c i) t -> p c t i", i=RUN), in_=rows.rearrange("p t (c i) -> p c t i", i=RUN))

@@ -284,15 +284,15 @@ def tile_multiheadlatentattention_pb_kernel(tc, x, Wkva, kv_a_norm_w, Wkvb, out_
                     )
 
         def sum_squares(i):
-            col = slice(i, i + 1)
             squares = stage.tile([P, LATENT], BF16)
             nc.scalar.activation(
                 out=squares[:], in_=latent_ps[i][:], func=ACT.Square, scale=1.0 / math.sqrt(LATENT),
-                accum_out=mean_sq[:, col],
+                accum_out=mean_sq[:, i : i + 1],
             )
-            nc.gpsimd.tensor_scalar(
-                out=mean_eps[:, col], in0=mean_sq[:, col], scalar1=1.0, scalar2=EPS, op0=ALU.mult, op1=ALU.add
-            )
+
+        def inverse_root(i):
+            col = slice(i, i + 1)
+            nc.vector.tensor_scalar_add(out=mean_eps[:, col], in0=mean_sq[:, col], scalar1=EPS)
             nc.gpsimd.tensor_tensor(out=rstd[:, col], in0=mean_eps[:, col], in1=minus_half[:], op=ALU.pow)
 
         def scale(i):
@@ -362,9 +362,9 @@ def tile_multiheadlatentattention_pb_kernel(tc, x, Wkva, kv_a_norm_w, Wkvb, out_
                 op=ALU.add,
             )
 
-        def spread(b, n):
+        def spread(b, n, copy):
             k_tiles[(b, n)] = keep.tile([P, GROUP_HEADS, ROWS, D_NOPE + D_ROPE], F32, name="k_tile%d%d" % (b, n))
-            nc.vector.tensor_copy(
+            copy(
                 out=k_tiles[(b, n)][:, :, 0, D_NOPE:],
                 in_=rotated[0][:, b, :].unsqueeze(1).to_broadcast([P, GROUP_HEADS, D_ROPE]),
             )
@@ -481,19 +481,22 @@ def tile_multiheadlatentattention_pb_kernel(tc, x, Wkva, kv_a_norm_w, Wkvb, out_
         store_odd_rope(1)
         regroup_nope(0, nc.scalar.copy)
         sum_squares(0)
+        inverse_root(0)
         regroup_v(0, LAST_HEADS, nc.vector.tensor_copy)
         sum_squares(1)
+        inverse_root(1)
         for c in range(3):
             latent_pass(c, 3)
+        rope_passes(0)
         latent_pass(3, 2)
         latent_pass(3, 3)
-        rope_passes(0)
         scale(0)
         regroup_v(0, FIRST_HEADS, nc.scalar.copy)
         transpose_h(0)
         rotate_cos(0)
         scale(1)
         sum_squares(2)
+        inverse_root(2)
         transpose_h(1)
         copy_h(0)
         quantise_v(0)
@@ -505,27 +508,30 @@ def tile_multiheadlatentattention_pb_kernel(tc, x, Wkva, kv_a_norm_w, Wkvb, out_
         copy_v(0, 0, 0)
         quantise_h(1)
         product_v(0, 0, 1)
-        quantise_nope(0)
+        inverse_root(3)
+        rotate_add(0)
         copy_v(0, 0, 1)
         send_v(0, 0)
-        product_nope(0, 0)
         scale(2)
         transpose_h(2)
+        quantise_nope(0)
+        product_nope(0, 0)
+        spread(0, 0, nc.scalar.copy)
         scale(3)
-        transpose_h(3)
         copy_h(2)
-        rotate_add(0)
-        spread(0, 0)
-        copy_h(3)
-        store_k(0, 0)
+        transpose_h(3)
         quantise_h(2)
-        quantise_h(3)
         product_v(0, 1, 0)
-        product_v(0, 1, 1)
-        spread(1, 0)
-        store_v(0, 1)
-        product_nope(0, 1)
+        store_k(0, 0)
+        copy_h(3)
         regroup_v(1, FIRST_HEADS, nc.vector.tensor_copy)
+        copy_v(0, 1, 0)
+        quantise_h(3)
+        product_v(0, 1, 1)
+        copy_v(0, 1, 1)
+        send_v(0, 1)
+        spread(1, 0, nc.vector.tensor_copy)
+        product_nope(0, 1)
         regroup_v(1, LAST_HEADS, nc.vector.tensor_copy)
         quantise_v(1)
         store_k(0, 1)
@@ -534,11 +540,11 @@ def tile_multiheadlatentattention_pb_kernel(tc, x, Wkva, kv_a_norm_w, Wkvb, out_
         store_v(1, 0)
         product_v(1, 1, 0)
         product_v(1, 1, 1)
-        spread(0, 1)
+        spread(0, 1, nc.vector.tensor_copy)
         store_v(1, 1)
         regroup_nope(1, nc.vector.tensor_copy)
         quantise_nope(1)
-        spread(1, 1)
+        spread(1, 1, nc.vector.tensor_copy)
         product_nope(1, 0)
         store_k(1, 0)
         product_nope(1, 1)

import math
from contextlib import ExitStack

import concourse.mybir as mybir
from concourse.masks import make_identity

F32 = mybir.dt.float32
BF16 = mybir.dt.bfloat16
I32 = mybir.dt.int32
U32 = mybir.dt.uint32
U8 = mybir.dt.uint8
FP8X4 = mybir.dt.float8_e4m3fn_x4
ALU = mybir.AluOpType
ACT = mybir.ActivationFunctionType

P = 128
PACK = 4
K_PASS = P * PACK

BATCH, SEQ, D_MODEL = 2, 256, 2048
HEADS, D_NOPE, D_ROPE, D_V = 16, 64, 128, 128
LATENT = 512
A_COLS = LATENT + D_ROPE
HEAD_COLS = D_NOPE + D_V
THETA = 10000.0
EPS = 1e-6

A_PASSES = D_MODEL // K_PASS
ROWS = SEQ // P
TILES = BATCH * ROWS
GROUP_HEADS = 4
GROUPS = HEADS // GROUP_HEADS
GROUP_COLS = GROUP_HEADS * HEAD_COLS
V_COLS = GROUP_HEADS * D_V
NOPE_COLS = GROUP_HEADS * D_NOPE
VECTOR_COLS = (576, 384, 352, 352)
FREQS = D_ROPE // 2
FINE = 8
RUN = 4

K_RUN = D_NOPE + D_ROPE + D_NOPE
FIRST_HEADS, LAST_HEADS = slice(0, GROUP_HEADS // 2), slice(GROUP_HEADS // 2, GROUP_HEADS)
ALL_HEADS = slice(0, GROUP_HEADS)

ROUND_MAGIC = 1.5 * 2.0**23
COS, SIN = 0, 1

FLOPS = 2 * BATCH * SEQ * (D_MODEL * A_COLS + LATENT * HEADS * HEAD_COLS)


def tile_multiheadlatentattention_pb_kernel(tc, x, Wkva, kv_a_norm_w, Wkvb, out_0, out_1):
    nc = tc.nc
    with ExitStack() as ctx:
        const = ctx.enter_context(tc.tile_pool(name="const", bufs=1))
        raw = ctx.enter_context(tc.tile_pool(name="raw", bufs=1))
        keep = ctx.enter_context(tc.tile_pool(name="keep", bufs=1))
        stage = ctx.enter_context(tc.tile_pool(name="stage", bufs=2))
        per_tile = ctx.enter_context(tc.tile_pool(name="per_tile", bufs=TILES))
        psum = ctx.enter_context(tc.psum_pool(name="psum", bufs=1))
        ctx.enter_context(tc.manual_schedule())

        def bank_hold(shape, dtype, name):
            return psum.tile(shape, dtype, tag="hold", bufs=5, name=name)

        def bank_pass(shape, dtype, name):
            return psum.tile(shape, dtype, tag="pass", bufs=3, name=name)

        def quantise(codes, scales, grouped):
            nc.vector.quantize_mx(out=codes.bitcast(FP8X4), scales=scales, in_=grouped)

        def mx_pass(out, lhs_codes, lhs_scales, rhs_codes, rhs_scales, start, stop):
            nc.tensor.matmul_mx(
                out=out,
                lhsT=lhs_codes.bitcast(FP8X4),
                lhsT_scale=lhs_scales,
                rhs=rhs_codes.bitcast(FP8X4),
                rhs_scale=rhs_scales,
                start=start,
                stop=stop,
            )

        wa_raw = {}
        x_raw = {}
        wb_raw = {}

        def load_wa(c):
            wa_raw[c] = raw.tile([P, PACK, A_COLS], BF16, name="wa_raw%d" % c)
            nc.sync.dma_start(
                out=wa_raw[c][:], in_=Wkva[c * K_PASS : (c + 1) * K_PASS, :].rearrange("(p t) n -> p t n", t=PACK)
            )

        def load_x(i):
            b, j = divmod(i, ROWS)
            x_raw[i] = raw.tile([P, D_MODEL], BF16, name="x_raw%d" % i)
            nc.sync.dma_start(out=x_raw[i][:], in_=x[b].rearrange("(p j) d -> p j d", j=ROWS)[:, j, :])

        def load_wb(g):
            wb_raw[g] = raw.tile([P, PACK, GROUP_COLS], BF16, name="wb_raw%d" % g)
            nc.sync.dma_start(
                out=wb_raw[g][:],
                in_=Wkvb[:, g * GROUP_COLS : (g + 1) * GROUP_COLS].rearrange("(p t) n -> p t n", t=PACK),
            )

        pos = const.tile([P, ROWS], F32)
        nc.gpsimd.iota(
            pos[:], pattern=[[1, ROWS]], base=0, channel_multiplier=ROWS, allow_small_or_imprecise_dtypes=True
        )
        zero_col = const.tile([P, 1], F32)
        nc.gpsimd.memset(zero_col[:], 0.0)
        ident_f32 = const.tile([P, P], F32)
        make_identity(nc, ident_f32[:])
        gain_row = const.tile([P, LATENT], BF16)
        nc.gpsimd.memset(gain_row[:], 0.0)
        load_wa(0)
        load_x(0)
        load_x(1)
        load_wa(1)
        nc.sync.dma_start(out=gain_row[0:1, :], in_=kv_a_norm_w.rearrange("(o n) -> o n", o=1))
        load_x(2)
        load_wa(2)
        load_x(3)
        load_wa(3)
        for g in range(GROUPS):
            load_wb(g)

        minus_half = const.tile([P, 1], F32)
        nc.gpsimd.memset(minus_half[:], -0.5)
        ones = const.tile([P, P], BF16)
        nc.gpsimd.memset(ones[:], 1.0)

        warm = const.tile([P, 1], F32)
        nc.scalar.activation(out=warm[:], in_=zero_col[:], func=ACT.Sin)
        factors = const.tile([P, 2, FINE], F32)
        nc.vector.memset(factors[:], 1.0)
        for level in range(3):
            bit = 2**level
            for part_of_f, unit in ((0, FINE), (1, 1)):
                has_bit = factors[:, part_of_f, :].rearrange("p (m two c) -> p m two c", two=2, c=bit)[:, :, 1, :]
                nc.vector.tensor_scalar_mul(out=has_bit, in0=has_bit, scalar1=THETA ** (-bit * unit / 64.0))
        per_pos = const.tile([P, FREQS], F32)
        nc.vector.scalar_tensor_tensor(
            out=per_pos[:].rearrange("p (a b) -> p a b", b=FINE),
            in0=factors[:, 0, :].unsqueeze(2).to_broadcast([P, FINE, FINE]), scalar=1.0 / (2.0 * math.pi),
            in1=factors[:, 1, :].unsqueeze(1).to_broadcast([P, FINE, FINE]), op0=ALU.mult, op1=ALU.mult,
        )
        turns = const.tile([P, ROWS, FREQS], F32)
        for j in range(ROWS):
            nc.vector.tensor_scalar(
                out=turns[:, j, :], in0=per_pos[:], scalar1=pos[:, j : j + 1], scalar2=None, op0=ALU.mult
            )
        whole = const.tile([P, ROWS, FREQS], F32)
        nc.vector.tensor_scalar(
            out=whole[:], in0=turns[:], scalar1=ROUND_MAGIC, scalar2=ROUND_MAGIC, op0=ALU.add, op1=ALU.subtract
        )
        part = const.tile([P, ROWS, FREQS], F32)
        nc.vector.tensor_tensor(out=part[:], in0=turns[:], in1=whole[:], op=ALU.subtract)
        size = const.tile([P, ROWS, FREQS], F32)
        table = const.tile([P, 2, ROWS, D_ROPE], F32)

        x_codes = keep.tile([P, TILES, A_PASSES * P], U32, align_bytes=64)
        x_scales = keep.tile([P, TILES, A_PASSES * P], U8, align_bytes=64)
        wa_codes = keep.tile([P, A_PASSES, A_COLS], U32, align_bytes=64)
        wa_scales = keep.tile([P, A_PASSES, A_COLS], U8, align_bytes=64)
        h_codes = keep.tile([P, TILES * P], U32, align_bytes=64)
        h_scales = keep.tile([P, TILES * P], U8, align_bytes=64)
        wv_codes = keep.tile([P, GROUPS, V_COLS], U32, align_bytes=64)
        wv_scales = keep.tile([P, GROUPS, V_COLS], U8, align_bytes=64)
        wn_codes = keep.tile([P, GROUPS, NOPE_COLS], U32, align_bytes=64)
        wn_scales = keep.tile([P, GROUPS, NOPE_COLS], U8, align_bytes=64)
        mean_sq = const.tile([P, TILES], F32)
        mean_eps = const.tile([P, TILES], F32)
        rstd = const.tile([P, TILES], F32)
        gain = const.tile([P, LATENT], F32)
        h_grouped = keep.tile([P, TILES, P, PACK], BF16, align_bytes=64)

        wa_grouped = {}
        xT_ps = {}
        x_grouped = {}
        gain_ps = {}
        latent_ps = {}
        rope_ps = {}
        h_tiles = {}
        hT_ps = {}
        wv_grouped = {}
        wn_grouped = {}
        by_cos = {}
        by_sin = {}
        rotated = {}
        v_ps = {}
        nope_ps = {}
        k_tiles = {}
        v_tiles = {}

        def sin_table():
            nc.scalar.activation(out=size[:], in_=part[:], func=ACT.Abs)
            nc.scalar.activation(
                out=table[:, COS, :, :].rearrange("p j (h f) -> p j h f", h=2),
                in_=size[:].unsqueeze(2).to_broadcast([P, ROWS, 2, FREQS]),
                func=ACT.Sin, scale=-2.0 * math.pi, bias=math.pi / 2.0,
            )
            for e, sign in ((0, 1.0), (1, -1.0)):
                nc.scalar.activation(
                    out=table[:, SIN, :, :].rearrange("p j (h m e) -> p j h m e", h=2, e=2)[:, :, :, :, e],
                    in_=part[:].rearrange("p j (m e) -> p j m e", e=2)[:, :, :, 1 - e]
                    .unsqueeze(2).to_broadcast([P, ROWS, 2, FREQS // 2]),
                    func=ACT.Sin, scale=sign * 2.0 * math.pi,
                )

        def interleave(copy, out, rows):
            copy(out=out.rearrange("p (c i) t -> p c t i", i=RUN), in_=rows.rearrange("p t (c i) -> p c t i", i=RUN))

        def regroup_wa(c):
            wa_grouped[c] = stage.tile([P, A_COLS, PACK], BF16, align_bytes=64, name="wa_grouped%d" % c, tag="wa_grouped")
            cols = slice(0, VECTOR_COLS[c])
            interleave(nc.vector.tensor_copy, wa_grouped[c][:, cols, :], wa_raw[c][:, :, cols])

        def copy_wa(c):
            cols = slice(VECTOR_COLS[c], A_COLS)
            interleave(nc.scalar.copy, wa_grouped[c][:, cols, :], wa_raw[c][:, :, cols])

        def quantise_wa(c, cols):
            quantise(
                wa_codes[:, c, cols], wa_scales[:, c, cols], wa_grouped[c][:, cols, :].rearrange("p n t -> p (n t)")
            )

        def quantise_latent(c):
            quantise_wa(c, slice(0, LATENT))

        def quantise_rope(c):
            quantise_wa(c, slice(LATENT, A_COLS))

        def transpose_x(i):
            x_words = x_raw[i][:].bitcast(F32)
            for half in range(2):
                xT_ps[(i, half)] = bank_pass([P, 2, 2, P], F32, "xT_ps%d%d" % (i, half))
                for c2 in range(2):
                    for u in range(2):
                        w0 = (2 * half + c2) * 2 * P
                        nc.tensor.transpose(
                            xT_ps[(i, half)][:, c2, u, :], x_words[:, w0 + u : w0 + 2 * P : 2], ident_f32[:]
                        )

        def copy_x(i, half):
            if half == 0:
                x_grouped[i] = per_tile.tile([P, A_PASSES * P * PACK], BF16, align_bytes=64, name="x_grouped%d" % i, tag="x_grouped")
            xg_words = x_grouped[i][:].bitcast(F32).rearrange("p (c r u) -> p c r u", c=A_PASSES, u=2)
            nc.scalar.copy(
                out=xg_words[:, 2 * half : 2 * half + 2, :, :],
                in_=xT_ps[(i, half)][:].rearrange("p c u r -> p c r u"),
            )

        def quantise_x(i, halves=(0, 2)):
            words = slice(halves[0] * 2 * P, halves[1] * 2 * P)
            quantise(
                x_codes[:, i, words], x_scales[:, i, words], x_grouped[i][:, words.start * PACK : words.stop * PACK]
            )

        def gain_product():
            gain_ps["all"] = bank_pass([P, LATENT], F32, "gain_ps")
            nc.tensor.matmul(out=gain_ps["all"][:], lhsT=ones[:], rhs=gain_row[:], start=True, stop=True)

        def gain_copy():
            nc.scalar.copy(out=gain[:], in_=gain_ps["all"][:])

        def latent_pass(c, i):
            if c == 0:
                latent_ps[i] = bank_hold([P, LATENT], F32, "latent_ps%d" % i)
            toks = slice(c * P, (c + 1) * P)
            mx_pass(
                latent_ps[i][:], x_codes[:, i, toks], x_scales[:, i, toks],
                wa_codes[:, c, 0:LATENT], wa_scales[:, c, 0:LATENT], start=(c == 0), stop=(c == A_PASSES - 1),
            )

        def rope_passes(j):
            rope_ps[j] = bank_hold([P, BATCH, D_ROPE], F32, "rope_ps%d" % j)
            for b in range(BATCH):
                i = b * ROWS + j
                for c in range(A_PASSES):
                    toks = slice(c * P, (c + 1) * P)
                    mx_pass(
                        rope_ps[j][:, b, :], x_codes[:, i, toks], x_scales[:, i, toks],
                        wa_codes[:, c, LATENT:A_COLS], wa_scales[:, c, LATENT:A_COLS],
                        start=(c == 0), stop=(c == A_PASSES - 1),
                    )

        def sum_squares(i):
            squares = stage.tile([P, LATENT], BF16)
            nc.scalar.activation(
                out=squares[:], in_=latent_ps[i][:], func=ACT.Square, scale=1.0 / math.sqrt(LATENT),
                accum_out=mean_sq[:, i : i + 1],
            )

        def inverse_root(i):
            col = slice(i, i + 1)
            nc.vector.tensor_scalar_add(out=mean_eps[:, col], in0=mean_sq[:, col], scalar1=EPS)
            nc.gpsimd.tensor_tensor(out=rstd[:, col], in0=mean_eps[:, col], in1=minus_half[:], op=ALU.pow)

        def scale(i):
            h_tiles[i] = per_tile.tile([P, LATENT], BF16, name="h%d" % i, tag="h")
            nc.vector.scalar_tensor_tensor(
                out=h_tiles[i][:], in0=latent_ps[i][:], scalar=rstd[:, i : i + 1], in1=gain[:], op0=ALU.mult, op1=ALU.mult
            )

        def transpose_h(i):
            h_words = h_tiles[i][:].bitcast(F32)
            hT_ps[i] = bank_pass([P, 2, P], F32, "hT_ps%d" % i)
            for u in range(2):
                nc.tensor.transpose(hT_ps[i][:, u, :], h_words[:, u : 2 * P : 2], ident_f32[:])

        def copy_h(i):
            nc.scalar.copy(
                out=h_grouped[:, i, :, :].rearrange("p r t -> p (r t)").bitcast(F32).rearrange("p (r u) -> p r u", u=2),
                in_=hT_ps[i][:].rearrange("p u r -> p r u"),
            )

        def quantise_h(i):
            toks = slice(i * P, (i + 1) * P)
            quantise(h_codes[:, toks], h_scales[:, toks], h_grouped[:, i, :, :].rearrange("p r t -> p (r t)"))

        def regroup_nope(g, copy):
            wn_grouped[g] = stage.tile([P, NOPE_COLS, PACK], BF16, align_bytes=64, name="wn_grouped%d" % g, tag="wn_grouped")
            by_head = wb_raw[g][:].rearrange("p t (h f) -> p h t f", f=HEAD_COLS)
            copy(
                out=wn_grouped[g][:].rearrange("p (h c i) t -> p h c t i", h=GROUP_HEADS, i=RUN),
                in_=by_head[:, :, :, 0:D_NOPE].rearrange("p h t (c i) -> p h c t i", i=RUN),
            )

        def regroup_v(g, heads, copy):
            if g not in wv_grouped:
                wv_grouped[g] = stage.tile([P, V_COLS * PACK], BF16, align_bytes=64, name="wv_grouped%d" % g, tag="wv_grouped")
            by_head = wb_raw[g][:].rearrange("p t (h f) -> p h t f", f=HEAD_COLS)
            copy(
                out=wv_grouped[g][:].rearrange("p (h c i t) -> p h c t i", h=GROUP_HEADS, i=RUN, t=PACK)[:, heads],
                in_=by_head[:, heads, :, D_NOPE:].rearrange("p h t (c i) -> p h c t i", i=RUN),
            )

        def quantise_v(g):
            quantise(wv_codes[:, g, :], wv_scales[:, g, :], wv_grouped[g][:])

        def quantise_nope(g):
            quantise(wn_codes[:, g, :], wn_scales[:, g, :], wn_grouped[g][:].rearrange("p n t -> p (n t)"))

        def times_table(j, which, products):
            products[j] = stage.tile([P, BATCH, D_ROPE], F32, name="product%d%d" % (which, j), tag="product%d" % which)
            nc.vector.tensor_tensor(
                out=products[j][:], in0=rope_ps[j][:],
                in1=table[:, which, j, :].unsqueeze(1).to_broadcast([P, BATCH, D_ROPE]), op=ALU.mult,
            )

        def rotate_cos(j):
            times_table(j, COS, by_cos)

        def rotate_sin(j):
            times_table(j, SIN, by_sin)

        def rotate_add(j):
            rotated[j] = keep.tile([P, BATCH, D_ROPE], F32, name="rotated%d" % j)
            nc.vector.tensor_tensor(
                out=rotated[j][:].rearrange("p b (m e) -> p (b m) e", e=2),
                in0=by_cos[j][:].rearrange("p b (m e) -> p (b m) e", e=2),
                in1=by_sin[j][:].rearrange("p b (m e) -> p (b m) e", e=2)[:, :, ::-1],
                op=ALU.add,
            )

        def spread(b, n, copy):
            k_tiles[(b, n)] = keep.tile([P, GROUP_HEADS, ROWS, D_NOPE + D_ROPE], F32, name="k_tile%d%d" % (b, n))
            copy(
                out=k_tiles[(b, n)][:, :, 0, D_NOPE:],
                in_=rotated[0][:, b, :].unsqueeze(1).to_broadcast([P, GROUP_HEADS, D_ROPE]),
            )

        def store_odd_rope(b):
            nc.sync.dma_start(
                out=out_0[b].rearrange("h (p j) f -> p h j f", j=ROWS)[:, :, 1, D_NOPE:],
                in_=rotated[1][:, b, :].unsqueeze(1).to_broadcast([P, HEADS, D_ROPE]),
            )

        def tokens(b, j):
            return slice((b * ROWS + j) * P, (b * ROWS + j + 1) * P)

        def product_v(g, b, j):
            toks = tokens(b, j)
            v_ps[(g, b, j)] = bank_pass([P, V_COLS], F32, "v_ps%d%d%d" % (g, b, j))
            mx_pass(
                v_ps[(g, b, j)][:], h_codes[:, toks], h_scales[:, toks],
                wv_codes[:, g, :], wv_scales[:, g, :], start=True, stop=True,
            )

        def product_nope(g, b):
            nope_ps[(g, b)] = bank_hold([P, ROWS, NOPE_COLS], F32, "nope_ps%d%d" % (g, b))
            for j in range(ROWS):
                toks = tokens(b, j)
                mx_pass(
                    nope_ps[(g, b)][:, j, :], h_codes[:, toks], h_scales[:, toks],
                    wn_codes[:, g, :], wn_scales[:, g, :], start=True, stop=True,
                )

        def copy_v(g, b, j):
            if (g, b) not in v_tiles:
                v_tiles[(g, b)] = per_tile.tile([P, GROUP_HEADS, ROWS, D_V], F32, name="v_tile%d%d" % (g, b), tag="v_tile")
            nc.scalar.copy(
                out=v_tiles[(g, b)][:, :, j, :], in_=v_ps[(g, b, j)][:].rearrange("p (h f) -> p h f", h=GROUP_HEADS)
            )

        def send_v(g, b):
            heads = slice(g * GROUP_HEADS, (g + 1) * GROUP_HEADS)
            nc.sync.dma_start(
                out=out_1[b, heads].rearrange("h (p j) f -> p h (j f)", j=ROWS),
                in_=v_tiles[(g, b)][:].rearrange("p h j f -> p h (j f)"),
            )

        def store_v(g, b):
            for j in range(ROWS):
                copy_v(g, b, j)
            send_v(g, b)

        def store_k(g, b):
            heads = slice(g * GROUP_HEADS, (g + 1) * GROUP_HEADS)
            k_tile = k_tiles[(b, g % 2)]
            nc.scalar.copy(
                out=k_tile[:, :, :, 0:D_NOPE],
                in_=nope_ps[(g, b)][:].rearrange("p j (h f) -> p h j f", h=GROUP_HEADS),
            )
            nc.sync.dma_start(
                out=out_0[b, heads].rearrange("h (p j) f -> p h (j f)", j=ROWS)[:, :, 0:K_RUN],
                in_=k_tile[:].rearrange("p h j f -> p h (j f)")[:, :, 0:K_RUN],
            )

        regroup_wa(0)
        copy_wa(0)
        sin_table()
        transpose_x(0)
        copy_x(0, 0)
        copy_x(0, 1)
        quantise_rope(0)
        quantise_latent(0)
        transpose_x(1)
        copy_x(1, 0)
        quantise_x(0, (0, 1))
        quantise_x(0, (1, 2))
        copy_x(1, 1)
        regroup_wa(1)
        copy_wa(1)
        quantise_x(1)
        transpose_x(2)
        latent_pass(0, 0)
        quantise_rope(1)
        quantise_latent(1)
        copy_x(2, 0)
        copy_x(2, 1)
        latent_pass(0, 1)
        latent_pass(1, 0)
        regroup_wa(2)
        copy_wa(2)
        quantise_x(2)
        transpose_x(3)
        copy_x(3, 0)
        copy_x(3, 1)
        gain_product()
        latent_pass(1, 1)
        latent_pass(0, 2)
        latent_pass(1, 2)
        quantise_rope(2)
        quantise_latent(2)
        regroup_wa(3)
        copy_wa(3)
        quantise_x(3)
        quantise_rope(3)
        latent_pass(2, 0)
        latent_pass(2, 1)
        latent_pass(2, 2)
        rope_passes(1)
        quantise_latent(3)
        latent_pass(3, 0)
        latent_pass(3, 1)
        gain_copy()
        rotate_cos(1)
        rotate_sin(1)
        rotate_add(1)
        store_odd_rope(0)
        store_odd_rope(1)
        regroup_nope(0, nc.scalar.copy)
        sum_squares(0)
        inverse_root(0)
        regroup_v(0, LAST_HEADS, nc.vector.tensor_copy)
        sum_squares(1)
        inverse_root(1)
        for c in range(3):
            latent_pass(c, 3)
        rope_passes(0)
        latent_pass(3, 2)
        latent_pass(3, 3)
        scale(0)
        regroup_v(0, FIRST_HEADS, nc.scalar.copy)
        transpose_h(0)
        rotate_cos(0)
        scale(1)
        sum_squares(2)
        inverse_root(2)
        transpose_h(1)
        copy_h(0)
        quantise_v(0)
        quantise_h(0)
        product_v(0, 0, 0)
        sum_squares(3)
        rotate_sin(0)
        copy_h(1)
        copy_v(0, 0, 0)
        quantise_h(1)
        product_v(0, 0, 1)
        inverse_root(3)
        rotate_add(0)
        copy_v(0, 0, 1)
        send_v(0, 0)
        scale(2)
        transpose_h(2)
        quantise_nope(0)
        product_nope(0, 0)
        spread(0, 0, nc.scalar.copy)
        scale(3)
        copy_h(2)
        transpose_h(3)
        quantise_h(2)
        product_v(0, 1, 0)
        store_k(0, 0)
        copy_h(3)
        regroup_v(1, FIRST_HEADS, nc.vector.tensor_copy)
        copy_v(0, 1, 0)
        quantise_h(3)
        product_v(0, 1, 1)
        copy_v(0, 1, 1)
        send_v(0, 1)
        spread(1, 0, nc.vector.tensor_copy)
        product_nope(0, 1)
        regroup_v(1, LAST_HEADS, nc.vector.tensor_copy)
        quantise_v(1)
        store_k(0, 1)
        product_v(1, 0, 0)
        product_v(1, 0, 1)
        store_v(1, 0)
        product_v(1, 1, 0)
        product_v(1, 1, 1)
        spread(0, 1, nc.vector.tensor_copy)
        store_v(1, 1)
        regroup_nope(1, nc.vector.tensor_copy)
        quantise_nope(1)
        spread(1, 1, nc.vector.tensor_copy)
        product_nope(1, 0)
        store_k(1, 0)
        product_nope(1, 1)
        store_k(1, 1)
        for g in range(2, 4):
            regroup_v(g, ALL_HEADS, nc.vector.tensor_copy)
            regroup_nope(g, nc.vector.tensor_copy)
            quantise_v(g)
            quantise_nope(g)
            for b in range(2):
                product_v(g, b, 0)
                product_v(g, b, 1)
                product_nope(g, b)
                store_v(g, b)
                store_k(g, b)
